import numpy as np
import ml_dtypes


def mxq(x, axis, fmt="e4m3"):
    dtype, down = {"e4m3": (ml_dtypes.float8_e4m3fn, 7), "e5m2": (ml_dtypes.float8_e5m2, 14)}[fmt]
    v = np.moveaxis(np.asarray(x, np.float32).astype(ml_dtypes.bfloat16).astype(np.float64), axis, -1)
    blocks = v.reshape(v.shape[:-1] + (-1, 32))
    amax = np.abs(blocks).max(-1, keepdims=True)
    byte = np.maximum(np.where(amax > 0, np.frexp(amax)[1] - 1 + 127, 0) - down, 1)
    scale = np.exp2(byte - 127.0)
    codes = (blocks / scale).astype(np.float32).astype(dtype).astype(np.float64)
    return np.moveaxis((codes * scale).reshape(v.shape), -1, axis)


WIDE = False


def mx_kscale(k):
    if not WIDE:
        return np.ones(k)
    levels = np.array([18, -18])
    if k % 512:
        return np.exp2(np.random.permutation(np.resize(levels, k // 32))).repeat(32)
    a = np.empty((k // 512, 16))
    for p in range(k // 512):
        a[p, :8] = np.random.permutation(np.resize(levels, 8))
        for g in range(8):
            far = levels[np.abs(levels - a[p, g]) >= 10]
            a[p, g + 8] = far[np.random.randint(len(far))]
    return np.exp2(a.ravel()).repeat(32)


BF16 = ml_dtypes.bfloat16


def bf(x):
    return np.asarray(x, np.float32).astype(BF16)


def f64(x):
    return np.asarray(x).astype(np.float64)


B, V, E, M = 512, 4096, 512, 1024


def setup_inputs():
    s = mx_kscale(B)[:, None]
    u = mx_kscale(V)
    v = mx_kscale(2 * M)
    vs, vi = v[:M], v[M:]
    y2_0 = bf(np.maximum(np.random.standard_normal((B, E)), 0.0))
    first = bf(np.random.standard_normal((B, M)) * 0.4 * (vs / vi))
    ws_0 = bf(np.random.standard_normal((M, E)) * 1.4 / np.sqrt(E))
    b_second = bf(np.random.standard_normal(M) * 0.3)
    wi_0 = bf(np.random.standard_normal((M, E)) * 1.4 / np.sqrt(E))
    b_int = bf(np.random.standard_normal(M) * 0.3)
    w_out = bf(np.random.standard_normal((V, M)) / np.sqrt(M) * vi[None, :] / u[:, None])
    b_out = bf(np.random.standard_normal(V) * 0.3)
    g = bf(np.random.standard_normal((B, V)) * np.exp2(np.random.randint(-6, 1, (B, 1))) / s * u)
    z_second = f64(y2_0) @ f64(ws_0).T + f64(b_second)
    z_int = f64(y2_0) @ f64(wi_0).T + f64(b_int)
    return {"y2": bf(f64(y2_0) * s),
            "first": first,
            "w_second": bf(f64(ws_0) / vs[:, None]),
            "b_second": b_second,
            "w_int": bf(f64(wi_0) / vi[:, None]),
            "b_int": b_int,
            "w_out": w_out,
            "b_out": b_out,
            "z_second": np.asarray(z_second, np.float32),
            "z_int": np.asarray(z_int, np.float32),
            "grad_out": g}


def reference(y2, first, w_second, b_second, w_int, b_int, w_out, b_out, z_second, z_int, grad_out):
    dh = mxq(f64(grad_out), 1, "e5m2") @ mxq(f64(w_out), 0, "e4m3")
    d_second = dh * f64(first) * (f64(z_second) > 0.0)
    d_int = dh * (f64(z_int) > 0.0)
    dz1 = np.concatenate([d_second, d_int], axis=1)
    w1 = np.concatenate([f64(w_second), f64(w_int)], axis=0)
    dy2 = mxq(dz1, 1, "e5m2") @ mxq(w1, 0, "e4m3")
    dw_second = mxq(d_second, 0, "e5m2").T @ mxq(f64(y2), 0, "e4m3")
    return dy2, dw_second

@@ -1,0 +1,300 @@
+from contextlib import ExitStack
+
+import concourse.mybir as mybir
+from concourse.masks import make_identity
+
+TOK, V, E, M = 512, 4096, 512, 1024
+FLOPS = 2 * (TOK * V * M + TOK * 2 * M * E + M * TOK * E)
+BYTES = 2 * (TOK * E + TOK * M + 2 * M * E + V * M + TOK * V) + 4 * (2 * TOK * M + TOK * E + M * E)
+
+F32 = mybir.dt.float32
+BF16 = mybir.dt.bfloat16
+U32 = mybir.dt.uint32
+U8 = mybir.dt.uint8
+E4M3 = mybir.dt.float8_e4m3fn_x4
+E5M2 = mybir.dt.float8_e5m2_x4
+MULT = mybir.AluOpType.mult
+ADD = mybir.AluOpType.add
+IS_GT = mybir.AluOpType.is_gt
+
+P = 128
+H = 512
+
+
+def tile_smcrossbaby_1_pb_v_kernel(
+    tc, y2, first, w_second, b_second, w_int, b_int, w_out, b_out, z_second, z_int, grad_out, out_0, out_1
+):
+    nc = tc.nc
+    v_copy = nc.vector.tensor_copy
+    s_copy = nc.scalar.copy
+
+    with ExitStack() as ctx:
+        keep = ctx.enter_context(tc.tile_pool(name="keep", bufs=1))
+        big = ctx.enter_context(tc.tile_pool(name="big", bufs=7))
+        small = ctx.enter_context(tc.tile_pool(name="small", bufs=5))
+        groups = ctx.enter_context(tc.tile_pool(name="groups", bufs=8))
+        outs = ctx.enter_context(tc.tile_pool(name="outs", bufs=6))
+        psum = ctx.enter_context(tc.psum_pool(name="psum", bufs=1))
+
+        ident = keep.tile([P, P], F32, name="ident")
+        make_identity(nc, ident[:])
+
+        ctx.enter_context(tc.manual_schedule())
+
+        def codes_and_scales(name, width):
+            codes = keep.tile([P, width], U32, name=name + "_codes", align_bytes=64)
+            scales = keep.tile([P, width], U8, name=name + "_scales", align_bytes=64)
+            return codes, scales
+
+        w_q = codes_and_scales("w", 8 * M)
+        g_q = codes_and_scales("g", 8 * TOK)
+        y_q = codes_and_scales("y", E)
+        w1_q = codes_and_scales("w1", 4 * E)
+        dt_q = codes_and_scales("dt", M)
+        df_q = codes_and_scales("df", 4 * TOK)
+
+        def load(pool, src, name):
+            raw = pool.tile(list(src.shape), src.dtype, name=name, tag="raw", align_bytes=64)
+            nc.sync.dma_start(out=raw[:], in_=src)
+            return raw
+
+        def new_group():
+            return groups.tile([P, 4 * H], BF16, name="group", align_bytes=64)
+
+        def interleave(copy, group, src, c0, c1):
+            dst = group[:, 4 * c0 : 4 * c1].rearrange("p (c i t) -> p c t i", i=4, t=4)
+            copy(out=dst, in_=src[:, :, c0:c1].rearrange("p t (c i) -> p c t i", i=4))
+
+        def quantize(group, q, c0, fmt):
+            nc.vector.quantize_mx(
+                out=q[0][:, c0 : c0 + H].bitcast(fmt), scales=q[1][:, c0 : c0 + H], in_=group[:]
+            )
+
+        def bank(n, shape):
+            return psum.tile(shape, F32, name=f"bank{n}", tag=f"bank{n}")
+
+        def mx(out, lhs, l0, lfmt, rhs, r0, start, stop):
+            nc.tensor.matmul_mx(
+                out=out[:],
+                lhsT=lhs[0][:, l0 : l0 + P].bitcast(lfmt),
+                lhsT_scale=lhs[1][:, l0 : l0 + P],
+                rhs=rhs[0][:, r0 : r0 + H].bitcast(E4M3),
+                rhs_scale=rhs[1][:, r0 : r0 + H],
+                start=start,
+                stop=stop,
+            )
+
+        def transpose_pairs(words, j0, w0, b):
+            ps = bank(b, [P, 2, 2, P])
+            for j in range(2):
+                for u in range(2):
+                    nc.tensor.transpose(ps[:, j, u, :], words[:, j0 + j, w0 + u : w0 + 256 : 2], ident[:])
+            return ps
+
+        def untangle(copy, group, h, ps):
+            dst = group[:, 1024 * h : 1024 * (h + 1)].bitcast(F32).rearrange("p (j r u) -> p j r u", j=2, u=2)
+            copy(out=dst, in_=ps[:].rearrange("p j u r -> p j r u"))
+
+        g_hbm = grad_out.rearrange("(p j) v -> p j v", j=4)
+        w_hbm = w_out.rearrange("(k p j) m -> k p j m", p=P, j=4)
+        y_hbm = y2.rearrange("(p j) e -> p j e", j=4)
+        ws_hbm = w_second.rearrange("(k p j) e -> p k j e", p=P, j=4)
+        wi_hbm = w_int.rearrange("(k p j) e -> p k j e", p=P, j=4)
+        f_hbm = first.rearrange("(p j) m -> p j m", j=4)
+        zs_hbm = z_second.rearrange("(p j) m -> p j m", j=4)
+        zi_hbm = z_int.rearrange("(p j) m -> p j m", j=4)
+
+        g_raw = {}
+        w_raw = {}
+        g0 = load(small, g_hbm[:, :, 0:H], "g0")
+        w0a = load(small, w_hbm[0][:, :, 0:H], "w0a")
+        g1 = load(small, g_hbm[:, :, H : 2 * H], "g1")
+        w0b = load(small, w_hbm[0][:, :, H:M], "w0b")
+        g_raw[0] = (g0, 0)
+        g_raw[1] = (g1, 0)
+        w_raw[0] = (w0a[:], w0b[:])
+
+        def load_g(k):
+            t = load(big, g_hbm[:, :, H * k : H * (k + 2)], f"g{k}")
+            g_raw[k] = (t, 0)
+            g_raw[k + 1] = (t, 256)
+
+        def load_w(i):
+            t = load(big, w_hbm[i], f"w{i}")
+            w_raw[i] = (t[:, :, 0:H], t[:, :, H:M])
+
+        load_g(2)
+        load_w(1)
+        load_g(4)
+        load_w(2)
+        load_g(6)
+        load_w(3)
+        load_w(4)
+        y_raw = load(small, y_hbm, "y")
+        load_w(5)
+        ws_raw = load(big, ws_hbm, "ws")
+        load_w(6)
+        fa_raw = load(small, f_hbm[:, :, 0:H], "fa")
+        zsa_raw = load(big, zs_hbm[:, :, 0:H], "zsa")
+        load_w(7)
+        zia_raw = load(big, zi_hbm[:, :, 0:H], "zia")
+        fb_raw = load(small, f_hbm[:, :, H:M], "fb")
+        zsb_raw = load(big, zs_hbm[:, :, H:M], "zsb")
+        zib_raw = load(big, zi_hbm[:, :, H:M], "zib")
+        wi_raw = load(big, wi_hbm, "wi")
+
+        dh_a = [bank(t, [P, H]) for t in range(4)]
+        g_ps = {}
+        ga = {}
+        gb = {}
+
+        def transpose_g(k):
+            raw, w0 = g_raw[k]
+            words = raw[:].bitcast(F32)
+            g_ps[k] = [transpose_pairs(words, 2 * h, w0, 4 + 2 * (k % 2) + h) for h in range(2)]
+
+        def matmul_dh(dh, half, i):
+            for t in range(4):
+                mx(dh[t], g_q, TOK * i + P * t, E5M2, w_q, M * i + H * half, i == 0, i == 7)
+
+        def quantize_w(i, half, group):
+            quantize(group, w_q, M * i + H * half, E4M3)
+
+        transpose_g(0)
+        transpose_g(1)
+        for i in range(4):
+            ga[i] = new_group()
+            interleave(v_copy, ga[i], w_raw[i][0], 0, H)
+            gg = [new_group(), new_group()]
+            for k in range(2):
+                for h in range(2):
+                    untangle(s_copy, gg[k], h, g_ps[2 * i + k][h])
+            if i > 0:
+                quantize_w(i - 1, 1, gb[i - 1])
+                matmul_dh(dh_a, 0, i - 1)
+            if i < 3:
+                transpose_g(2 * i + 2)
+                transpose_g(2 * i + 3)
+            gb[i] = new_group()
+            interleave(s_copy, gb[i], w_raw[i][1], 0, H)
+            for k in range(2):
+                quantize(gg[k], g_q, TOK * (2 * i + k), E5M2)
+            quantize_w(i, 0, ga[i])
+
+        dh_b = [bank(4 + t, [P, H]) for t in range(4)]
+
+        def step(i, passes_b):
+            ga[i] = new_group()
+            gb[i] = new_group()
+            interleave(v_copy, ga[i], w_raw[i][0], 0, H)
+            interleave(s_copy, gb[i], w_raw[i][1], 0, H)
+            quantize_w(i - 1, 1, gb[i - 1])
+            quantize_w(i, 0, ga[i])
+            matmul_dh(dh_a, 0, i - 1)
+            for b in passes_b:
+                matmul_dh(dh_b, 1, b)
+
+        fs = [keep.tile([P, 4, H], BF16, name=f"fs{h}") for h in range(2)]
+
+        def gate(half, z, f):
+            for t in (0, 2):
+                nc.vector.scalar_tensor_tensor(
+                    out=fs[half][:, t : t + 2, :], in0=z[:, t : t + 2, :], scalar=0.0, in1=f[:, t : t + 2, :],
+                    op0=IS_GT, op1=MULT,
+                )
+
+        step(4, (0, 1, 2))
+        gy = new_group()
+        interleave(s_copy, gy, y_raw[:], 0, H)
+        step(5, (3,))
+        quantize(gy, y_q, 0, E4M3)
+        gw = [new_group(), new_group()]
+        interleave(v_copy, gw[0], ws_raw[:, 0], 0, H)
+        interleave(s_copy, gw[1], ws_raw[:, 1], 0, H)
+        step(6, (4,))
+        quantize(gw[0], w1_q, 0, E4M3)
+        gate(0, zsa_raw, fa_raw)
+        step(7, (5,))
+        quantize(gw[1], w1_q, E, E4M3)
+        quantize_w(7, 1, gb[7])
+        matmul_dh(dh_a, 0, 7)
+        matmul_dh(dh_b, 1, 6)
+        matmul_dh(dh_b, 1, 7)
+
+        ds = [keep.tile([P, 4, H], BF16, name=f"ds{h}", align_bytes=64) for h in range(2)]
+        di = [keep.tile([P, 4, H], BF16, name=f"di{h}", align_bytes=64) for h in range(2)]
+        dh = [dh_a, dh_b]
+        zi = [zia_raw, zib_raw]
+
+        def elementwise(half, t):
+            nc.vector.tensor_tensor(out=ds[half][:, t, :], in0=dh[half][t][:], in1=fs[half][:, t, :], op=MULT)
+            nc.vector.scalar_tensor_tensor(
+                out=di[half][:, t, :], in0=zi[half][:, t, :], scalar=0.0, in1=dh[half][t][:], op0=IS_GT, op1=MULT
+            )
+
+        def transpose_d(half, h):
+            return [
+                transpose_pairs(d[half][:].bitcast(F32), 2 * h, 0, 4 * half + 2 * h + n) for n, d in enumerate((ds, di))
+            ]
+
+        def dw_tiles(half, copies):
+            for c in range(4):
+                ps = bank(4 * half + c, [P, H])
+                mx(ps, dt_q, H * half + P * c, E5M2, y_q, 0, True, True)
+                o = outs.tile([P, H], F32, name="dw")
+                copies[c](out=o[:], in_=ps[:])
+                r0 = H * half + P * c
+                nc.sync.dma_start(out=out_1[r0 : r0 + P, :], in_=o[:])
+
+        fg = [[new_group(), new_group()], None]
+        elementwise(0, 0)
+        elementwise(0, 1)
+        ps01 = transpose_d(0, 0)
+        untangle(s_copy, fg[0][0], 0, ps01[0])
+        untangle(s_copy, fg[0][1], 0, ps01[1])
+        elementwise(0, 2)
+        elementwise(0, 3)
+        ps23 = transpose_d(0, 1)
+        untangle(s_copy, fg[0][0], 1, ps23[0])
+        untangle(s_copy, fg[0][1], 1, ps23[1])
+        gate(1, zsb_raw, fb_raw)
+        tg0 = new_group()
+        interleave(s_copy, tg0, ds[0][:], 0, H)
+        quantize(fg[0][0], df_q, 0, E5M2)
+        elementwise(1, 0)
+        quantize(fg[0][1], df_q, 2 * TOK, E5M2)
+        elementwise(1, 1)
+        quantize(tg0, dt_q, 0, E5M2)
+        fg[1] = [new_group(), new_group()]
+        ps01 = transpose_d(1, 0)
+        dw_tiles(0, [s_copy] * 4)
+        untangle(s_copy, fg[1][0], 0, ps01[0])
+        untangle(s_copy, fg[1][1], 0, ps01[1])
+        elementwise(1, 2)
+        elementwise(1, 3)
+        ps23 = transpose_d(1, 1)
+        gi = [new_group(), new_group()]
+        interleave(v_copy, gi[0], wi_raw[:, 0], 0, H)
+        interleave(s_copy, gi[1], wi_raw[:, 1], 0, H)
+        untangle(s_copy, fg[1][0], 1, ps23[0])
+        untangle(s_copy, fg[1][1], 1, ps23[1])
+        quantize(gi[0], w1_q, 2 * E, E4M3)
+        quantize(gi[1], w1_q, 3 * E, E4M3)
+        dy = [bank(t, [P, H]) for t in range(4)]
+        for t in range(4):
+            mx(dy[t], df_q, P * t, E5M2, w1_q, 0, True, False)
+        for t in range(4):
+            mx(dy[t], df_q, 2 * TOK + P * t, E5M2, w1_q, 2 * E, False, False)
+        tg1 = new_group()
+        interleave(s_copy, tg1, ds[1][:], 0, H)
+        quantize(fg[1][0], df_q, TOK, E5M2)
+        quantize(fg[1][1], df_q, 3 * TOK, E5M2)
+        quantize(tg1, dt_q, H, E5M2)
+        o0_hbm = out_0.rearrange("(p j) e -> p j e", j=4)
+        for t in range(4):
+            mx(dy[t], df_q, TOK + P * t, E5M2, w1_q, E, False, False)
+            mx(dy[t], df_q, 3 * TOK + P * t, E5M2, w1_q, 3 * E, False, True)
+            o = outs.tile([P, H], F32, name="dw")
+            (v_copy if t % 2 == 0 else s_copy)(out=o[:], in_=dy[t][:])
+            nc.sync.dma_start(out=o0_hbm[:, t, :], in_=o[:])
+        dw_tiles(1, [v_copy, s_copy, v_copy, s_copy])

@@ -19,26 +19,47 @@ IS_GT = mybir.AluOpType.is_gt
 
 P = 128
 H = 512
+LOADS = "w5 g0 w0b g1 w1 g2 w2 g4 w3 g6 fb w0a w4 w7 w6 zsb fa zsa y wi zia ws zib"
+ORDER = """
+Iw5a.0/V//0 Iw5a.1/S// Iw5b.1/V//1 Tg0.0//0/ Iw5b.0/S// Qw5a/// Tg0.1//1/ Cg0.0/V//2 Iw0b.1/S//3 Iw0b.0/V//
+Tg1.0//2/ Qw5b/// Cg0.1/S// Qw0b/// Tg1.1//3/ Cg1.0/S//4 Qg0/// Cg1.1/S// Iw1a.0/V//5 Mb0//4,5,6,7/
+Iw1a.1/S// Qg1/// Iw1b.1/V//6 Iw1b.0/S// Qw1a/// Tg3.1//0/ Qw1b/// Tg2.1//1/ Cg3.1/S//7 Tg2.0//2/ Cg2.1/V//0
+Mb1/// Cg2.0/V// Iw2a.0/S//1 Iw2b.1/V//3 Iw2b.0/V// Iw2a.1/S// Tg3.0//3/ Qg2/// Qw2b/// Tg4.0//0/ Cg3.0/S//
+Qw2a/// Tg5.0//1/ Cg4.0/S//2 Tg4.1//2/ Qg3/// Cg5.0/S//4 Tg5.1//3/ Cg4.1/S// Iw3a.1/V//5 Iw3b.0/S//6 Qg4///
+Mb2/// Cg5.1/V// Iw3a.0/S// Iw3b.1/V// Qg5/// Tg7.1//0/ Tg6.0//1/ Qw3b/// Cg7.1/S//0 Tg6.1//2/ Qw3a///
+Cg6.0/S//3 Tg7.0//3/ Iw0a.1/S//1 Cg6.1/V// Iw0a.0/V// Mb3/// Cg7.0/S// Qg6/// Qw0a/// Iw4b.0/S//7 Iw4b.1/V//
+Ma0//0,1,2,3/ Iw4a.0/V//2 Qw4b/// Iw7a.1/S//4 Ma1/// Iw7b.1/V//6 Qg7/// Mb4/// Iw7b.0/S// Iw4a.1/V// Mb5///
+Iw7a.0/V// Iw6a.1/S//5 Qw7b/// Ma2/// Qw7a/// Iw6b.1/S//3 Qw4a/// Ma3/// Fb0/// Iw6a.0/S// Ma4/// Fb1///
+Iw6b.0/S// Ma5/// Qw6a/// Qw6b/// Ma6/// Fa1/// Iy.0/S//1 Ma7/// Fa0/// Iy.1/S// Mb6/// Ea2/// Ii1.1/G//7
+Ea3/// Mb7/// Ii1.0/S// Ea1/// Ea0/// Ii0.1/G//0 Ii0.0/S// Eb2/// Xa2/// Ita.0/G//6 Ita.1/S// Xa1///
+Tdsa0//2/ Eb3/// Tdsa1//1/ Cdsa0/S//4 Qy/// Tdsb1//2/ Is0.1/S//2 Is1.0/G//5 Eb0/// Xa0/// Cdsb1/S//3 Eb1///
+Tdia0//0/ Is0.0/G// Is1.1/S// Xa3/// Tdsb0//2/ Xb1/// Itb.1/G//1 Itb.0/S// Xb0/// Tdia1//3/ Xb3/// Tdib0//5/
+Xb2/// Cdsb0/S// Qs0/// Tdib1//4/ Cdsa1/S// Qtb/// Cdib0/S//2 Cdib1/S// Qdsa/// Wb2//7/ Cdia1/S//1 Qta///
+Wb1//6/ Cdia0/S// Wb0//2/ Qi0/// Wa0//1/ Ob1/S// Wa3//5/ Qdia/// Wa2//4/ Oa0/S// Wa1//3/ Qi1/// Y1A//0/
+Oa2/S// Qdib/// Y2A//6/ Oa1/S// Qdsb/// Y0A//1/ Oa3/S// Qs1/// Y3A//4/ Ob2/S// Wb3//3/ Ob0/V// Y1B///
+Ob3/S// Y0B/// OY1/S// Y2B/// OY0/S// Y3B/// OY2/S// OY3/V//
+"""
 
 
 def tile_smcrossbaby_1_pb_v_kernel(
     tc, y2, first, w_second, b_second, w_int, b_int, w_out, b_out, z_second, z_int, grad_out, out_0, out_1
 ):
     nc = tc.nc
-    v_copy = nc.vector.tensor_copy
-    s_copy = nc.scalar.copy
+
+    def g_copy(out, in_):
+        nc.gpsimd.tensor_scalar(out=out, in0=in_, scalar1=1.0, scalar2=0.0, op0=MULT, op1=ADD)
+
+    copies = {"V": nc.vector.tensor_copy, "S": nc.scalar.copy, "G": g_copy}
 
     with ExitStack() as ctx:
         keep = ctx.enter_context(tc.tile_pool(name="keep", bufs=1))
         big = ctx.enter_context(tc.tile_pool(name="big", bufs=7))
-        small = ctx.enter_context(tc.tile_pool(name="small", bufs=5))
-        groups = ctx.enter_context(tc.tile_pool(name="groups", bufs=8))
-        outs = ctx.enter_context(tc.tile_pool(name="outs", bufs=6))
+        small = ctx.enter_context(tc.tile_pool(name="small", bufs=7))
+        outs = ctx.enter_context(tc.tile_pool(name="outs", bufs=8))
         psum = ctx.enter_context(tc.psum_pool(name="psum", bufs=1))
 
         ident = keep.tile([P, P], F32, name="ident")
         make_identity(nc, ident[:])
-
         ctx.enter_context(tc.manual_schedule())
 
         def codes_and_scales(name, width):
@@ -52,48 +73,8 @@ def tile_smcrossbaby_1_pb_v_kernel(
         w1_q = codes_and_scales("w1", 4 * E)
         dt_q = codes_and_scales("dt", M)
         df_q = codes_and_scales("df", 4 * TOK)
-
-        def load(pool, src, name):
-            raw = pool.tile(list(src.shape), src.dtype, name=name, tag="raw", align_bytes=64)
-            nc.sync.dma_start(out=raw[:], in_=src)
-            return raw
-
-        def new_group():
-            return groups.tile([P, 4 * H], BF16, name="group", align_bytes=64)
-
-        def interleave(copy, group, src, c0, c1):
-            dst = group[:, 4 * c0 : 4 * c1].rearrange("p (c i t) -> p c t i", i=4, t=4)
-            copy(out=dst, in_=src[:, :, c0:c1].rearrange("p t (c i) -> p c t i", i=4))
-
-        def quantize(group, q, c0, fmt):
-            nc.vector.quantize_mx(
-                out=q[0][:, c0 : c0 + H].bitcast(fmt), scales=q[1][:, c0 : c0 + H], in_=group[:]
-            )
-
-        def bank(n, shape):
-            return psum.tile(shape, F32, name=f"bank{n}", tag=f"bank{n}")
-
-        def mx(out, lhs, l0, lfmt, rhs, r0, start, stop):
-            nc.tensor.matmul_mx(
-                out=out[:],
-                lhsT=lhs[0][:, l0 : l0 + P].bitcast(lfmt),
-                lhsT_scale=lhs[1][:, l0 : l0 + P],
-                rhs=rhs[0][:, r0 : r0 + H].bitcast(E4M3),
-                rhs_scale=rhs[1][:, r0 : r0 + H],
-                start=start,
-                stop=stop,
-            )
-
-        def transpose_pairs(words, j0, w0, b):
-            ps = bank(b, [P, 2, 2, P])
-            for j in range(2):
-                for u in range(2):
-                    nc.tensor.transpose(ps[:, j, u, :], words[:, j0 + j, w0 + u : w0 + 256 : 2], ident[:])
-            return ps
-
-        def untangle(copy, group, h, ps):
-            dst = group[:, 1024 * h : 1024 * (h + 1)].bitcast(F32).rearrange("p (j r u) -> p j r u", j=2, u=2)
-            copy(out=dst, in_=ps[:].rearrange("p j u r -> p j r u"))
+        ds = [keep.tile([P, 4, H], BF16, name=f"ds{h}", align_bytes=64) for h in range(2)]
+        di = [keep.tile([P, 4, H], BF16, name=f"di{h}", align_bytes=64) for h in range(2)]
 
         g_hbm = grad_out.rearrange("(p j) v -> p j v", j=4)
         w_hbm = w_out.rearrange("(k p j) m -> k p j m", p=P, j=4)
@@ -103,198 +84,148 @@ def tile_smcrossbaby_1_pb_v_kernel(
         f_hbm = first.rearrange("(p j) m -> p j m", j=4)
         zs_hbm = z_second.rearrange("(p j) m -> p j m", j=4)
         zi_hbm = z_int.rearrange("(p j) m -> p j m", j=4)
+        o0_hbm = out_0.rearrange("(p j) e -> p j e", j=4)
+        halves = {"a": slice(0, H), "b": slice(H, M)}
+        sources = {"y": y_hbm, "ws": ws_hbm, "wi": wi_hbm, "w0a": w_hbm[0][:, :, 0:H], "w0b": w_hbm[0][:, :, H:M]}
+        sources["g0"] = g_hbm[:, :, 0:H]
+        sources["g1"] = g_hbm[:, :, H : 2 * H]
+        for k in (2, 4, 6):
+            sources[f"g{k}"] = g_hbm[:, :, H * k : H * (k + 2)]
+        for i in range(1, 8):
+            sources[f"w{i}"] = w_hbm[i]
+        for c in "ab":
+            sources["f" + c] = f_hbm[:, :, halves[c]]
+            sources["zs" + c] = zs_hbm[:, :, halves[c]]
+            sources["zi" + c] = zi_hbm[:, :, halves[c]]
+        raw = {}
+        for n in LOADS.split():
+            pool = small if n in ("g0", "g1", "w0a", "w0b", "y", "fa", "fb") else big
+            raw[n] = pool.tile(list(sources[n].shape), sources[n].dtype, name="raw_" + n, tag="raw", align_bytes=64)
+            nc.sync.dma_start(out=raw[n][:], in_=sources[n])
 
-        g_raw = {}
-        w_raw = {}
-        g0 = load(small, g_hbm[:, :, 0:H], "g0")
-        w0a = load(small, w_hbm[0][:, :, 0:H], "w0a")
-        g1 = load(small, g_hbm[:, :, H : 2 * H], "g1")
-        w0b = load(small, w_hbm[0][:, :, H:M], "w0b")
-        g_raw[0] = (g0, 0)
-        g_raw[1] = (g1, 0)
-        w_raw[0] = (w0a[:], w0b[:])
+        view = {"y": raw["y"][:], "w0a": raw["w0a"][:], "w0b": raw["w0b"][:]}
+        for i in range(1, 8):
+            for c in "ab":
+                view[f"w{i}{c}"] = raw[f"w{i}"][:, :, halves[c]]
+        for k in range(2):
+            view[f"s{k}"] = raw["ws"][:, k]
+            view[f"i{k}"] = raw["wi"][:, k]
+        view["ta"] = ds[0][:]
+        view["tb"] = ds[1][:]
 
-        def load_g(k):
-            t = load(big, g_hbm[:, :, H * k : H * (k + 2)], f"g{k}")
-            g_raw[k] = (t, 0)
-            g_raw[k + 1] = (t, 256)
+        group = {}
+        ps = {}
+        dh = {}
 
-        def load_w(i):
-            t = load(big, w_hbm[i], f"w{i}")
-            w_raw[i] = (t[:, :, 0:H], t[:, :, H:M])
+        def bank(n, shape):
+            return psum.tile(shape, F32, name=f"bank{n}", tag=f"bank{n}")
 
-        load_g(2)
-        load_w(1)
-        load_g(4)
-        load_w(2)
-        load_g(6)
-        load_w(3)
-        load_w(4)
-        y_raw = load(small, y_hbm, "y")
-        load_w(5)
-        ws_raw = load(big, ws_hbm, "ws")
-        load_w(6)
-        fa_raw = load(small, f_hbm[:, :, 0:H], "fa")
-        zsa_raw = load(big, zs_hbm[:, :, 0:H], "zsa")
-        load_w(7)
-        zia_raw = load(big, zi_hbm[:, :, 0:H], "zia")
-        fb_raw = load(small, f_hbm[:, :, H:M], "fb")
-        zsb_raw = load(big, zs_hbm[:, :, H:M], "zsb")
-        zib_raw = load(big, zi_hbm[:, :, H:M], "zib")
-        wi_raw = load(big, wi_hbm, "wi")
-
-        dh_a = [bank(t, [P, H]) for t in range(4)]
-        g_ps = {}
-        ga = {}
-        gb = {}
-
-        def transpose_g(k):
-            raw, w0 = g_raw[k]
-            words = raw[:].bitcast(F32)
-            g_ps[k] = [transpose_pairs(words, 2 * h, w0, 4 + 2 * (k % 2) + h) for h in range(2)]
-
-        def matmul_dh(dh, half, i):
-            for t in range(4):
-                mx(dh[t], g_q, TOK * i + P * t, E5M2, w_q, M * i + H * half, i == 0, i == 7)
-
-        def quantize_w(i, half, group):
-            quantize(group, w_q, M * i + H * half, E4M3)
-
-        transpose_g(0)
-        transpose_g(1)
-        for i in range(4):
-            ga[i] = new_group()
-            interleave(v_copy, ga[i], w_raw[i][0], 0, H)
-            gg = [new_group(), new_group()]
-            for k in range(2):
-                for h in range(2):
-                    untangle(s_copy, gg[k], h, g_ps[2 * i + k][h])
-            if i > 0:
-                quantize_w(i - 1, 1, gb[i - 1])
-                matmul_dh(dh_a, 0, i - 1)
-            if i < 3:
-                transpose_g(2 * i + 2)
-                transpose_g(2 * i + 3)
-            gb[i] = new_group()
-            interleave(s_copy, gb[i], w_raw[i][1], 0, H)
-            for k in range(2):
-                quantize(gg[k], g_q, TOK * (2 * i + k), E5M2)
-            quantize_w(i, 0, ga[i])
-
-        dh_b = [bank(4 + t, [P, H]) for t in range(4)]
-
-        def step(i, passes_b):
-            ga[i] = new_group()
-            gb[i] = new_group()
-            interleave(v_copy, ga[i], w_raw[i][0], 0, H)
-            interleave(s_copy, gb[i], w_raw[i][1], 0, H)
-            quantize_w(i - 1, 1, gb[i - 1])
-            quantize_w(i, 0, ga[i])
-            matmul_dh(dh_a, 0, i - 1)
-            for b in passes_b:
-                matmul_dh(dh_b, 1, b)
-
-        fs = [keep.tile([P, 4, H], BF16, name=f"fs{h}") for h in range(2)]
-
-        def gate(half, z, f):
-            for t in (0, 2):
-                nc.vector.scalar_tensor_tensor(
-                    out=fs[half][:, t : t + 2, :], in0=z[:, t : t + 2, :], scalar=0.0, in1=f[:, t : t + 2, :],
-                    op0=IS_GT, op1=MULT,
-                )
-
-        step(4, (0, 1, 2))
-        gy = new_group()
-        interleave(s_copy, gy, y_raw[:], 0, H)
-        step(5, (3,))
-        quantize(gy, y_q, 0, E4M3)
-        gw = [new_group(), new_group()]
-        interleave(v_copy, gw[0], ws_raw[:, 0], 0, H)
-        interleave(s_copy, gw[1], ws_raw[:, 1], 0, H)
-        step(6, (4,))
-        quantize(gw[0], w1_q, 0, E4M3)
-        gate(0, zsa_raw, fa_raw)
-        step(7, (5,))
-        quantize(gw[1], w1_q, E, E4M3)
-        quantize_w(7, 1, gb[7])
-        matmul_dh(dh_a, 0, 7)
-        matmul_dh(dh_b, 1, 6)
-        matmul_dh(dh_b, 1, 7)
-
-        ds = [keep.tile([P, 4, H], BF16, name=f"ds{h}", align_bytes=64) for h in range(2)]
-        di = [keep.tile([P, 4, H], BF16, name=f"di{h}", align_bytes=64) for h in range(2)]
-        dh = [dh_a, dh_b]
-        zi = [zia_raw, zib_raw]
-
-        def elementwise(half, t):
-            nc.vector.tensor_tensor(out=ds[half][:, t, :], in0=dh[half][t][:], in1=fs[half][:, t, :], op=MULT)
-            nc.vector.scalar_tensor_tensor(
-                out=di[half][:, t, :], in0=zi[half][:, t, :], scalar=0.0, in1=dh[half][t][:], op0=IS_GT, op1=MULT
+        def quantize(g, q, c0, fmt):
+            nc.vector.quantize_mx(
+                out=q[0][:, c0 : c0 + H].bitcast(fmt), scales=q[1][:, c0 : c0 + H], in_=group[g][:]
             )
 
-        def transpose_d(half, h):
-            return [
-                transpose_pairs(d[half][:].bitcast(F32), 2 * h, 0, 4 * half + 2 * h + n) for n, d in enumerate((ds, di))
-            ]
+        def mx(out, lhs, l0, rhs, r0, start, stop):
+            nc.tensor.matmul_mx(
+                out=out[:],
+                lhsT=lhs[0][:, l0 : l0 + P].bitcast(E5M2),
+                lhsT_scale=lhs[1][:, l0 : l0 + P],
+                rhs=rhs[0][:, r0 : r0 + H].bitcast(E4M3),
+                rhs_scale=rhs[1][:, r0 : r0 + H],
+                start=start,
+                stop=stop,
+            )
 
-        def dw_tiles(half, copies):
-            for c in range(4):
-                ps = bank(4 * half + c, [P, H])
-                mx(ps, dt_q, H * half + P * c, E5M2, y_q, 0, True, True)
-                o = outs.tile([P, H], F32, name="dw")
-                copies[c](out=o[:], in_=ps[:])
-                r0 = H * half + P * c
-                nc.sync.dma_start(out=out_1[r0 : r0 + P, :], in_=o[:])
+        def transpose_pairs(words, j0, w0, t):
+            for j in range(2):
+                for u in range(2):
+                    nc.tensor.transpose(t[:, j, u, :], words[:, j0 + j, w0 + u : w0 + 256 : 2], ident[:])
 
-        fg = [[new_group(), new_group()], None]
-        elementwise(0, 0)
-        elementwise(0, 1)
-        ps01 = transpose_d(0, 0)
-        untangle(s_copy, fg[0][0], 0, ps01[0])
-        untangle(s_copy, fg[0][1], 0, ps01[1])
-        elementwise(0, 2)
-        elementwise(0, 3)
-        ps23 = transpose_d(0, 1)
-        untangle(s_copy, fg[0][0], 1, ps23[0])
-        untangle(s_copy, fg[0][1], 1, ps23[1])
-        gate(1, zsb_raw, fb_raw)
-        tg0 = new_group()
-        interleave(s_copy, tg0, ds[0][:], 0, H)
-        quantize(fg[0][0], df_q, 0, E5M2)
-        elementwise(1, 0)
-        quantize(fg[0][1], df_q, 2 * TOK, E5M2)
-        elementwise(1, 1)
-        quantize(tg0, dt_q, 0, E5M2)
-        fg[1] = [new_group(), new_group()]
-        ps01 = transpose_d(1, 0)
-        dw_tiles(0, [s_copy] * 4)
-        untangle(s_copy, fg[1][0], 0, ps01[0])
-        untangle(s_copy, fg[1][1], 0, ps01[1])
-        elementwise(1, 2)
-        elementwise(1, 3)
-        ps23 = transpose_d(1, 1)
-        gi = [new_group(), new_group()]
-        interleave(v_copy, gi[0], wi_raw[:, 0], 0, H)
-        interleave(s_copy, gi[1], wi_raw[:, 1], 0, H)
-        untangle(s_copy, fg[1][0], 1, ps23[0])
-        untangle(s_copy, fg[1][1], 1, ps23[1])
-        quantize(gi[0], w1_q, 2 * E, E4M3)
-        quantize(gi[1], w1_q, 3 * E, E4M3)
-        dy = [bank(t, [P, H]) for t in range(4)]
-        for t in range(4):
-            mx(dy[t], df_q, P * t, E5M2, w1_q, 0, True, False)
-        for t in range(4):
-            mx(dy[t], df_q, 2 * TOK + P * t, E5M2, w1_q, 2 * E, False, False)
-        tg1 = new_group()
-        interleave(s_copy, tg1, ds[1][:], 0, H)
-        quantize(fg[1][0], df_q, TOK, E5M2)
-        quantize(fg[1][1], df_q, 3 * TOK, E5M2)
-        quantize(tg1, dt_q, H, E5M2)
-        o0_hbm = out_0.rearrange("(p j) e -> p j e", j=4)
-        for t in range(4):
-            mx(dy[t], df_q, TOK + P * t, E5M2, w1_q, E, False, False)
-            mx(dy[t], df_q, 3 * TOK + P * t, E5M2, w1_q, 3 * E, False, True)
-            o = outs.tile([P, H], F32, name="dw")
-            (v_copy if t % 2 == 0 else s_copy)(out=o[:], in_=dy[t][:])
-            nc.sync.dma_start(out=o0_hbm[:, t, :], in_=o[:])
-        dw_tiles(1, [v_copy, s_copy, v_copy, s_copy])
+        def store(dst, src, copy):
+            o = outs.tile([P, H], F32, name="out_tile")
+            copy(out=o[:], in_=src[:])
+            nc.sync.dma_start(out=dst, in_=o[:])
+
+        for token in ORDER.split():
+            n, e, banks, slot = token.split("/")
+            banks = [int(b) for b in banks.split(",")] if banks else []
+            g = n[1:].split(".")[0]
+            if n[0:2] == "Cd":
+                g = n[1:4]
+            if slot:
+                group[g] = keep.tile([P, 4 * H], BF16, name="group" + slot, tag="group" + slot, align_bytes=64)
+            c = n[2] if len(n) > 2 else ""
+            half = 1 if c == "b" else 0
+            if n[0] == "I":
+                c0 = 256 * int(n[-1])
+                dst = group[g][:, 4 * c0 : 4 * (c0 + 256)].rearrange("p (c i t) -> p c t i", i=4, t=4)
+                copies[e](out=dst, in_=view[g][:, :, c0 : c0 + 256].rearrange("p t (c i) -> p c t i", i=4))
+            elif n[0] == "T":
+                ps[n[1:]] = bank(banks[0], [P, 2, 2, P])
+                if n[1] == "g":
+                    k = int(n[2])
+                    r = raw[f"g{k}"] if k < 2 else raw[f"g{k - k % 2}"]
+                    transpose_pairs(r[:].bitcast(F32), 2 * int(n[-1]), 256 * (k % 2) if k > 1 else 0, ps[n[1:]])
+                else:
+                    d = (ds if n[2] == "s" else di)[1 if n[3] == "b" else 0]
+                    transpose_pairs(d[:].bitcast(F32), 2 * int(n[-1]), 0, ps[n[1:]])
+            elif n[0] == "C":
+                h = int(n[-1])
+                dst = group[g][:, 1024 * h : 1024 * (h + 1)].bitcast(F32)
+                copies[e](
+                    out=dst.rearrange("p (j r u) -> p j r u", j=2, u=2), in_=ps[n[1:]][:].rearrange("p j u r -> p j r u")
+                )
+            elif n[0] == "Q":
+                if g[0] == "w":
+                    quantize(g, w_q, M * int(g[1]) + (H if g[2] == "b" else 0), E4M3)
+                elif g[0] == "g":
+                    quantize(g, g_q, TOK * int(g[1]), E5M2)
+                elif g == "y":
+                    quantize(g, y_q, 0, E4M3)
+                elif g[0] == "s":
+                    quantize(g, w1_q, E * int(g[1]), E4M3)
+                elif g[0] == "i":
+                    quantize(g, w1_q, E * (2 + int(g[1])), E4M3)
+                elif g[0] == "t":
+                    quantize(g, dt_q, H if g[1] == "b" else 0, E5M2)
+                else:
+                    quantize(g, df_q, TOK * ((2 if g[1] == "i" else 0) + (1 if g[2] == "b" else 0)), E5M2)
+            elif n[0] == "M":
+                i = int(n[2])
+                if i == 0:
+                    dh[n[1]] = [bank(b, [P, H]) for b in banks]
+                for t in range(4):
+                    mx(dh[n[1]][t], g_q, TOK * i + P * t, w_q, M * i + (H if n[1] == "b" else 0), i == 0, i == 7)
+            elif n[0] == "F":
+                t = 2 * int(n[2])
+                f = raw["f" + n[1]][:, t : t + 2, :]
+                nc.vector.scalar_tensor_tensor(
+                    out=f, in0=raw["zs" + n[1]][:, t : t + 2, :], scalar=0.0, in1=f, op0=IS_GT, op1=MULT
+                )
+            elif n[0] == "E":
+                t = int(n[2])
+                nc.vector.tensor_tensor(
+                    out=ds[n[1] == "b"][:, t, :], in0=dh[n[1]][t][:], in1=raw["f" + n[1]][:, t, :], op=MULT
+                )
+            elif n[0] == "X":
+                t = int(n[2])
+                nc.vector.scalar_tensor_tensor(
+                    out=di[n[1] == "b"][:, t, :], in0=raw["zi" + n[1]][:, t, :], scalar=0.0, in1=dh[n[1]][t][:],
+                    op0=IS_GT, op1=MULT,
+                )
+            elif n[0] == "W":
+                ps[n] = bank(banks[0], [P, H])
+                mx(ps[n], dt_q, (H if n[1] == "b" else 0) + P * int(n[2]), y_q, 0, True, True)
+            elif n[0:2] == "OY":
+                t = int(n[2])
+                store(o0_hbm[:, t, :], ps[f"Y{t}"], copies[e])
+            elif n[0] == "O":
+                r0 = (H if n[1] == "b" else 0) + P * int(n[2])
+                store(out_1[r0 : r0 + P, :], ps["W" + n[1:]], copies[e])
+            else:
+                t = int(n[1])
+                if n[2] == "A":
+                    ps[f"Y{t}"] = bank(banks[0], [P, H])
+                for a in (0, 2):
+                    k = a + (1 if n[2] == "B" else 0)
+                    mx(ps[f"Y{t}"], df_q, TOK * k + P * t, w1_q, E * k, k == 0, k == 3)

@@ -19,25 +19,35 @@ IS_GT = mybir.AluOpType.is_gt
 
 P = 128
 H = 512
-LOADS = "w5 g0 w0b g1 w1 g2 w2 g4 w3 g6 fb w0a w4 w7 w6 zsb fa zsa y wi zia ws zib"
-ORDER = """
-Iw5a.0/V//0 Iw5a.1/S// Iw5b.1/V//1 Tg0.0//0/ Iw5b.0/S// Qw5a/// Tg0.1//1/ Cg0.0/V//2 Iw0b.1/S//3 Iw0b.0/V//
-Tg1.0//2/ Qw5b/// Cg0.1/S// Qw0b/// Tg1.1//3/ Cg1.0/S//4 Qg0/// Cg1.1/S// Iw1a.0/V//5 Mb0//4,5,6,7/
-Iw1a.1/S// Qg1/// Iw1b.1/V//6 Iw1b.0/S// Qw1a/// Tg3.1//0/ Qw1b/// Tg2.1//1/ Cg3.1/S//7 Tg2.0//2/ Cg2.1/V//0
-Mb1/// Cg2.0/V// Iw2a.0/S//1 Iw2b.1/V//3 Iw2b.0/V// Iw2a.1/S// Tg3.0//3/ Qg2/// Qw2b/// Tg4.0//0/ Cg3.0/S//
-Qw2a/// Tg5.0//1/ Cg4.0/S//2 Tg4.1//2/ Qg3/// Cg5.0/S//4 Tg5.1//3/ Cg4.1/S// Iw3a.1/V//5 Iw3b.0/S//6 Qg4///
-Mb2/// Cg5.1/V// Iw3a.0/S// Iw3b.1/V// Qg5/// Tg7.1//0/ Tg6.0//1/ Qw3b/// Cg7.1/S//0 Tg6.1//2/ Qw3a///
-Cg6.0/S//3 Tg7.0//3/ Iw0a.1/S//1 Cg6.1/V// Iw0a.0/V// Mb3/// Cg7.0/S// Qg6/// Qw0a/// Iw4b.0/S//7 Iw4b.1/V//
-Ma0//0,1,2,3/ Iw4a.0/V//2 Qw4b/// Iw7a.1/S//4 Ma1/// Iw7b.1/V//6 Qg7/// Mb4/// Iw7b.0/S// Iw4a.1/V// Mb5///
-Iw7a.0/V// Iw6a.1/S//5 Qw7b/// Ma2/// Qw7a/// Iw6b.1/S//3 Qw4a/// Ma3/// Fb0/// Iw6a.0/S// Ma4/// Fb1///
-Iw6b.0/S// Ma5/// Qw6a/// Qw6b/// Ma6/// Fa1/// Iy.0/S//1 Ma7/// Fa0/// Iy.1/S// Mb6/// Ea2/// Ii1.1/G//7
-Ea3/// Mb7/// Ii1.0/S// Ea1/// Ea0/// Ii0.1/G//0 Ii0.0/S// Eb2/// Xa2/// Ita.0/G//6 Ita.1/S// Xa1///
-Tdsa0//2/ Eb3/// Tdsa1//1/ Cdsa0/S//4 Qy/// Tdsb1//2/ Is0.1/S//2 Is1.0/G//5 Eb0/// Xa0/// Cdsb1/S//3 Eb1///
-Tdia0//0/ Is0.0/G// Is1.1/S// Xa3/// Tdsb0//2/ Xb1/// Itb.1/G//1 Itb.0/S// Xb0/// Tdia1//3/ Xb3/// Tdib0//5/
-Xb2/// Cdsb0/S// Qs0/// Tdib1//4/ Cdsa1/S// Qtb/// Cdib0/S//2 Cdib1/S// Qdsa/// Wb2//7/ Cdia1/S//1 Qta///
-Wb1//6/ Cdia0/S// Wb0//2/ Qi0/// Wa0//1/ Ob1/S// Wa3//5/ Qdia/// Wa2//4/ Oa0/S// Wa1//3/ Qi1/// Y1A//0/
-Oa2/S// Qdib/// Y2A//6/ Oa1/S// Qdsb/// Y0A//1/ Oa3/S// Qs1/// Y3A//4/ Ob2/S// Wb3//3/ Ob0/V// Y1B///
-Ob3/S// Y0B/// OY1/S// Y2B/// OY0/S// Y3B/// OY2/S// OY3/V//
+GROUPS = 8
+
+LOADS = """
+y g0 w0a w1 g1 w3 w0b g2 w2 g4 w5 w4 g6 w6 zsb w7 fb zsa fa ws zia wi zib
+"""
+
+STEPS = """
+pack:y.1:V pack:y.0:S turn:g0.1:T quant:y.0:V pack:w0a.0:V pack:w0a.1:S turn:g0.0:T drain:g0.1:V drain:g0.0:V
+quant:w0a.0:V pack:w1a.0:S pack:w1a.1:V pack:w1b.0:V turn:g1.0:T pack:w1b.1:S quant:g0.0:V turn:g1.1:T
+quant:w1a.0:V drain:g1.0:V pack:w3a.1:S dh:a.0:T quant:w1b.0:V pack:w3b.0:V pack:w3a.0:S pack:w0b.1:V
+pack:w0b.0:V drain:g1.1:S quant:w3a.0:V pack:w3b.1:S turn:g3.0:T quant:g1.0:V turn:g2.0:T quant:w0b.0:V
+drain:g3.0:S dh:a.1:T quant:w3b.0:V drain:g2.0:S pack:w2a.1:V pack:w2b.1:S turn:g3.1:T pack:w2b.0:V pack:w2a.0:V
+turn:g2.1:T drain:g3.1:S quant:w2b.0:V turn:g4.1:T drain:g2.1:S quant:g3.0:V turn:g5.1:T drain:g4.1:S
+quant:g2.0:V turn:g5.0:T drain:g5.1:S quant:w2a.0:V turn:g4.0:T pack:w5b.1:S pack:w5b.0:V pack:w5a.0:V dh:a.2:T
+drain:g4.0:S quant:w5b.0:V pack:w5a.1:S pack:w4a.1:V quant:g4.0:V pack:w4b.1:S dh:a.3:T quant:w5a.0:V
+pack:w4b.0:V pack:w4a.0:S quant:w4b.0:V turn:g6.0:T drain:g5.0:S quant:w4a.0:V turn:g6.1:T drain:g6.0:V
+pack:w6b.1:S dh:a.4:T pack:w6a.0:V pack:w6a.1:V pack:w6b.0:S turn:g7.1:T quant:g5.0:V turn:g7.0:T quant:w6a.0:V
+drain:g6.1:S dh:a.5:T quant:w6b.0:V drain:g7.0:S quant:g6.0:V drain:g7.1:S quant:g7.0:V dh:b.0:T pack:w7a.0:S
+pack:w7b.1:V dh:a.6:T gate:b.0:V pack:w7b.0:S dh:b.1:T gate:b.1:V pack:w7a.1:S dh:b.2:T quant:w7b.0:V
+quant:w7a.0:V dh:b.3:T gate:a.0:V dh:a.7:T gate:a.1:V pack:s1.1:S dh:b.4:T pack:s0.1:G second:a.1:V second:a.2:V
+dh:b.5:T pack:s0.0:S second:a.0:V second:a.3:V dh:b.6:T pack:s1.0:S pack:ta.1:G int:a.2:V int:a.1:V dh:b.7:T
+pack:ta.0:S int:a.0:V pack:i0.1:G int:a.3:V turn:dia.0:T second:b.0:V pack:i1.1:S turn:dsa.0:T second:b.3:V
+turn:dsa.1:T pack:i0.0:G second:b.1:V turn:dia.1:T drain:dsa.1:S second:b.2:V drain:dia.1:S turn:dsb.0:T
+pack:tb.1:G int:b.0:V pack:tb.0:S turn:dsb.1:T int:b.2:V int:b.3:V drain:dia.0:S quant:ta.0:V turn:dib.1:T
+drain:dsa.0:S quant:tb.0:V pack:i1.0:S dw:a.1:T quant:s0.0:V dw:b.3:T quant:dia.0:V drain:dsb.1:S dw:a.2:T
+quant:i0.0:V dw_out:b.3:S dw:b.2:T int:b.1:V drain:dib.1:S dw:a.0:T dw:b.1:T quant:dsa.0:V dw_out:a.0:S
+turn:dib.0:T dw_out:a.2:S quant:s1.0:V dy:a.3:T dw_out:b.2:S drain:dsb.0:V dy:a.0:T dw_out:a.1:S quant:i1.0:V
+dw:a.3:T drain:dib.0:S dy:a.1:T quant:dsb.0:V dw_out:a.3:S dw:b.0:T quant:dib.0:V dy:a.2:T dw_out:b.1:S
+dw_out:b.0:V dy:b.1:T dy:b.3:T dy_out:b.1:S dy:b.2:T dy_out:b.3:S dy:b.0:T dy_out:b.2:S dy_out:b.0:V
 """
 
 
@@ -46,16 +56,16 @@ def tile_smcrossbaby_1_pb_v_kernel(
 ):
     nc = tc.nc
 
-    def g_copy(out, in_):
+    def gpsimd_copy(out, in_):
         nc.gpsimd.tensor_scalar(out=out, in0=in_, scalar1=1.0, scalar2=0.0, op0=MULT, op1=ADD)
 
-    copies = {"V": nc.vector.tensor_copy, "S": nc.scalar.copy, "G": g_copy}
+    copy_on = {"V": nc.vector.tensor_copy, "S": nc.scalar.copy, "G": gpsimd_copy}
 
     with ExitStack() as ctx:
         keep = ctx.enter_context(tc.tile_pool(name="keep", bufs=1))
         big = ctx.enter_context(tc.tile_pool(name="big", bufs=7))
         small = ctx.enter_context(tc.tile_pool(name="small", bufs=7))
-        outs = ctx.enter_context(tc.tile_pool(name="outs", bufs=8))
+        outs = ctx.enter_context(tc.tile_pool(name="outs", bufs=6))
         psum = ctx.enter_context(tc.psum_pool(name="psum", bufs=1))
 
         ident = keep.tile([P, P], F32, name="ident")
@@ -73,59 +83,84 @@ def tile_smcrossbaby_1_pb_v_kernel(
         w1_q = codes_and_scales("w1", 4 * E)
         dt_q = codes_and_scales("dt", M)
         df_q = codes_and_scales("df", 4 * TOK)
-        ds = [keep.tile([P, 4, H], BF16, name=f"ds{h}", align_bytes=64) for h in range(2)]
-        di = [keep.tile([P, 4, H], BF16, name=f"di{h}", align_bytes=64) for h in range(2)]
+        d_sec = [keep.tile([P, 4, H], BF16, name=f"d_sec{h}", align_bytes=64) for h in range(2)]
+        d_int = [keep.tile([P, 4, H], BF16, name=f"d_int{h}", align_bytes=64) for h in range(2)]
 
-        g_hbm = grad_out.rearrange("(p j) v -> p j v", j=4)
-        w_hbm = w_out.rearrange("(k p j) m -> k p j m", p=P, j=4)
-        y_hbm = y2.rearrange("(p j) e -> p j e", j=4)
-        ws_hbm = w_second.rearrange("(k p j) e -> p k j e", p=P, j=4)
-        wi_hbm = w_int.rearrange("(k p j) e -> p k j e", p=P, j=4)
-        f_hbm = first.rearrange("(p j) m -> p j m", j=4)
-        zs_hbm = z_second.rearrange("(p j) m -> p j m", j=4)
-        zi_hbm = z_int.rearrange("(p j) m -> p j m", j=4)
-        o0_hbm = out_0.rearrange("(p j) e -> p j e", j=4)
-        halves = {"a": slice(0, H), "b": slice(H, M)}
-        sources = {"y": y_hbm, "ws": ws_hbm, "wi": wi_hbm, "w0a": w_hbm[0][:, :, 0:H], "w0b": w_hbm[0][:, :, H:M]}
-        sources["g0"] = g_hbm[:, :, 0:H]
-        sources["g1"] = g_hbm[:, :, H : 2 * H]
+        by_token = "(p j) c -> p j c"
+        g_hbm, y_hbm, f_hbm, zs_hbm, zi_hbm, dy_hbm = (
+            x.rearrange(by_token, j=4) for x in (grad_out, y2, first, z_second, z_int, out_0)
+        )
+        w_hbm, ws_hbm, wi_hbm = (x.rearrange("(k p j) c -> p k j c", p=P, j=4) for x in (w_out, w_second, w_int))
+        cols = {"a": slice(0, H), "b": slice(H, M)}
+
+        hbm = {"y": y_hbm, "ws": ws_hbm, "wi": wi_hbm}
+        for k in (0, 1):
+            hbm[f"g{k}"] = g_hbm[:, :, H * k : H * (k + 1)]
         for k in (2, 4, 6):
-            sources[f"g{k}"] = g_hbm[:, :, H * k : H * (k + 2)]
+            hbm[f"g{k}"] = g_hbm[:, :, H * k : H * (k + 2)]
         for i in range(1, 8):
-            sources[f"w{i}"] = w_hbm[i]
+            hbm[f"w{i}"] = w_hbm[:, i]
         for c in "ab":
-            sources["f" + c] = f_hbm[:, :, halves[c]]
-            sources["zs" + c] = zs_hbm[:, :, halves[c]]
-            sources["zi" + c] = zi_hbm[:, :, halves[c]]
+            hbm["w0" + c] = w_hbm[:, 0, :, cols[c]]
+            hbm["f" + c] = f_hbm[:, :, cols[c]]
+            hbm["zs" + c] = zs_hbm[:, :, cols[c]]
+            hbm["zi" + c] = zi_hbm[:, :, cols[c]]
         raw = {}
         for n in LOADS.split():
-            pool = small if n in ("g0", "g1", "w0a", "w0b", "y", "fa", "fb") else big
-            raw[n] = pool.tile(list(sources[n].shape), sources[n].dtype, name="raw_" + n, tag="raw", align_bytes=64)
-            nc.sync.dma_start(out=raw[n][:], in_=sources[n])
+            half_size = n in ("g0", "g1", "w0a", "w0b", "y", "fa", "fb")
+            pool = small if half_size else big
+            raw[n] = pool.tile(list(hbm[n].shape), hbm[n].dtype, name="raw_" + n, tag="raw", align_bytes=64)
+            nc.sync.dma_start(out=raw[n][:], in_=hbm[n])
 
-        view = {"y": raw["y"][:], "w0a": raw["w0a"][:], "w0b": raw["w0b"][:]}
-        for i in range(1, 8):
-            for c in "ab":
-                view[f"w{i}{c}"] = raw[f"w{i}"][:, :, halves[c]]
+        rows_of = {"y": raw["y"][:], "ta": d_sec[0][:], "tb": d_sec[1][:]}
+        words_of = {}
+        dest = {"y": (y_q, 0, E4M3)}
+        for h, c in enumerate("ab"):
+            for i in range(8):
+                rows_of[f"w{i}{c}"] = raw["w0" + c][:] if i == 0 else raw[f"w{i}"][:, :, cols[c]]
+                dest[f"w{i}{c}"] = (w_q, M * i + H * h, E4M3)
+            words_of["ds" + c] = d_sec[h][:].bitcast(F32)
+            words_of["di" + c] = d_int[h][:].bitcast(F32)
+            dest["ds" + c] = (df_q, TOK * h, E5M2)
+            dest["di" + c] = (df_q, TOK * (2 + h), E5M2)
+            dest["t" + c] = (dt_q, H * h, E5M2)
+        for k in range(8):
+            words = raw[f"g{k}"][:] if k < 2 else raw[f"g{k - k % 2}"][:, :, H * (k % 2) : H * (k % 2 + 1)]
+            words_of[f"g{k}"] = words.bitcast(F32)
+            dest[f"g{k}"] = (g_q, TOK * k, E5M2)
         for k in range(2):
-            view[f"s{k}"] = raw["ws"][:, k]
-            view[f"i{k}"] = raw["wi"][:, k]
-        view["ta"] = ds[0][:]
-        view["tb"] = ds[1][:]
+            rows_of[f"s{k}"] = raw["ws"][:, k]
+            rows_of[f"i{k}"] = raw["wi"][:, k]
+            dest[f"s{k}"] = (w1_q, E * k, E4M3)
+            dest[f"i{k}"] = (w1_q, E * (2 + k), E4M3)
 
+        free_banks = list(range(8))
+        free_groups = list(range(GROUPS))
+        in_bank = {}
         group = {}
-        ps = {}
-        dh = {}
+        group_slot = {}
 
-        def bank(n, shape):
-            return psum.tile(shape, F32, name=f"bank{n}", tag=f"bank{n}")
+        def open_bank(key, shape):
+            n = free_banks[0]
+            free_banks.remove(n)
+            in_bank[key] = (psum.tile(shape, F32, name=f"bank{n}", tag=f"bank{n}"), n)
 
-        def quantize(g, q, c0, fmt):
-            nc.vector.quantize_mx(
-                out=q[0][:, c0 : c0 + H].bitcast(fmt), scales=q[1][:, c0 : c0 + H], in_=group[g][:]
-            )
+        def emptied(key):
+            tile, n = in_bank[key]
+            free_banks.append(n)
 
-        def mx(out, lhs, l0, rhs, r0, start, stop):
+        def bank(key):
+            return in_bank[key][0]
+
+        def group_of(key):
+            if key not in group:
+                n = free_groups[0]
+                free_groups.remove(n)
+                group_slot[key] = n
+                group[key] = keep.tile([P, 4 * H], BF16, name=f"group{n}", tag=f"group{n}", align_bytes=64)
+            return group[key]
+
+        def matmul(out, lhs, l0, rhs, r0, start, stop):
             nc.tensor.matmul_mx(
                 out=out[:],
                 lhsT=lhs[0][:, l0 : l0 + P].bitcast(E5M2),
@@ -136,96 +171,91 @@ def tile_smcrossbaby_1_pb_v_kernel(
                 stop=stop,
             )
 
-        def transpose_pairs(words, j0, w0, t):
+        def turn(what, n, engine):
+            open_bank(("turn", what, n), [P, 2, 2, P])
             for j in range(2):
                 for u in range(2):
-                    nc.tensor.transpose(t[:, j, u, :], words[:, j0 + j, w0 + u : w0 + 256 : 2], ident[:])
+                    nc.tensor.transpose(
+                        bank(("turn", what, n))[:, j, u, :], words_of[what][:, 2 * n + j, u : 256 : 2], ident[:]
+                    )
 
-        def store(dst, src, copy):
-            o = outs.tile([P, H], F32, name="out_tile")
-            copy(out=o[:], in_=src[:])
-            nc.sync.dma_start(out=dst, in_=o[:])
+        def drain(what, n, engine):
+            dst = group_of(what)[:, 2 * H * n : 2 * H * (n + 1)].bitcast(F32)
+            copy_on[engine](
+                out=dst.rearrange("p (j r u) -> p j r u", j=2, u=2),
+                in_=bank(("turn", what, n))[:].rearrange("p j u r -> p j r u"),
+            )
+            emptied(("turn", what, n))
 
-        for token in ORDER.split():
-            n, e, banks, slot = token.split("/")
-            banks = [int(b) for b in banks.split(",")] if banks else []
-            g = n[1:].split(".")[0]
-            if n[0:2] == "Cd":
-                g = n[1:4]
-            if slot:
-                group[g] = keep.tile([P, 4 * H], BF16, name="group" + slot, tag="group" + slot, align_bytes=64)
-            c = n[2] if len(n) > 2 else ""
-            half = 1 if c == "b" else 0
-            if n[0] == "I":
-                c0 = 256 * int(n[-1])
-                dst = group[g][:, 4 * c0 : 4 * (c0 + 256)].rearrange("p (c i t) -> p c t i", i=4, t=4)
-                copies[e](out=dst, in_=view[g][:, :, c0 : c0 + 256].rearrange("p t (c i) -> p c t i", i=4))
-            elif n[0] == "T":
-                ps[n[1:]] = bank(banks[0], [P, 2, 2, P])
-                if n[1] == "g":
-                    k = int(n[2])
-                    r = raw[f"g{k}"] if k < 2 else raw[f"g{k - k % 2}"]
-                    transpose_pairs(r[:].bitcast(F32), 2 * int(n[-1]), 256 * (k % 2) if k > 1 else 0, ps[n[1:]])
-                else:
-                    d = (ds if n[2] == "s" else di)[1 if n[3] == "b" else 0]
-                    transpose_pairs(d[:].bitcast(F32), 2 * int(n[-1]), 0, ps[n[1:]])
-            elif n[0] == "C":
-                h = int(n[-1])
-                dst = group[g][:, 1024 * h : 1024 * (h + 1)].bitcast(F32)
-                copies[e](
-                    out=dst.rearrange("p (j r u) -> p j r u", j=2, u=2), in_=ps[n[1:]][:].rearrange("p j u r -> p j r u")
-                )
-            elif n[0] == "Q":
-                if g[0] == "w":
-                    quantize(g, w_q, M * int(g[1]) + (H if g[2] == "b" else 0), E4M3)
-                elif g[0] == "g":
-                    quantize(g, g_q, TOK * int(g[1]), E5M2)
-                elif g == "y":
-                    quantize(g, y_q, 0, E4M3)
-                elif g[0] == "s":
-                    quantize(g, w1_q, E * int(g[1]), E4M3)
-                elif g[0] == "i":
-                    quantize(g, w1_q, E * (2 + int(g[1])), E4M3)
-                elif g[0] == "t":
-                    quantize(g, dt_q, H if g[1] == "b" else 0, E5M2)
-                else:
-                    quantize(g, df_q, TOK * ((2 if g[1] == "i" else 0) + (1 if g[2] == "b" else 0)), E5M2)
-            elif n[0] == "M":
-                i = int(n[2])
-                if i == 0:
-                    dh[n[1]] = [bank(b, [P, H]) for b in banks]
-                for t in range(4):
-                    mx(dh[n[1]][t], g_q, TOK * i + P * t, w_q, M * i + (H if n[1] == "b" else 0), i == 0, i == 7)
-            elif n[0] == "F":
-                t = 2 * int(n[2])
-                f = raw["f" + n[1]][:, t : t + 2, :]
-                nc.vector.scalar_tensor_tensor(
-                    out=f, in0=raw["zs" + n[1]][:, t : t + 2, :], scalar=0.0, in1=f, op0=IS_GT, op1=MULT
-                )
-            elif n[0] == "E":
-                t = int(n[2])
-                nc.vector.tensor_tensor(
-                    out=ds[n[1] == "b"][:, t, :], in0=dh[n[1]][t][:], in1=raw["f" + n[1]][:, t, :], op=MULT
-                )
-            elif n[0] == "X":
-                t = int(n[2])
-                nc.vector.scalar_tensor_tensor(
-                    out=di[n[1] == "b"][:, t, :], in0=raw["zi" + n[1]][:, t, :], scalar=0.0, in1=dh[n[1]][t][:],
-                    op0=IS_GT, op1=MULT,
-                )
-            elif n[0] == "W":
-                ps[n] = bank(banks[0], [P, H])
-                mx(ps[n], dt_q, (H if n[1] == "b" else 0) + P * int(n[2]), y_q, 0, True, True)
-            elif n[0:2] == "OY":
-                t = int(n[2])
-                store(o0_hbm[:, t, :], ps[f"Y{t}"], copies[e])
-            elif n[0] == "O":
-                r0 = (H if n[1] == "b" else 0) + P * int(n[2])
-                store(out_1[r0 : r0 + P, :], ps["W" + n[1:]], copies[e])
+        def pack(what, n, engine):
+            c0 = 256 * n
+            src = rows_of[what][:, :, c0 : c0 + 256]
+            dst = group_of(what)[:, 4 * c0 : 4 * (c0 + 256)]
+            if engine == "G":
+                gpsimd_copy(out=dst.rearrange("p (c t) -> p c t", t=4), in_=src.rearrange("p t c -> p c t"))
             else:
-                t = int(n[1])
-                if n[2] == "A":
-                    ps[f"Y{t}"] = bank(banks[0], [P, H])
-                for a in (0, 2):
-                    k = a + (1 if n[2] == "B" else 0)
-                    mx(ps[f"Y{t}"], df_q, TOK * k + P * t, w1_q, E * k, k == 0, k == 3)
+                copy_on[engine](
+                    out=dst.rearrange("p (c i t) -> p c t i", i=4, t=4), in_=src.rearrange("p t (c i) -> p c t i", i=4)
+                )
+
+        def quant(what, n, engine):
+            q, c0, fmt = dest[what]
+            nc.vector.quantize_mx(
+                out=q[0][:, c0 : c0 + H].bitcast(fmt), scales=q[1][:, c0 : c0 + H], in_=group[what][:]
+            )
+            free_groups.append(group_slot[what])
+
+        def dh(c, i, engine):
+            for t in range(4):
+                if i == 0:
+                    open_bank(("dh", c, t), [P, H])
+                matmul(bank(("dh", c, t)), g_q, TOK * i + P * t, w_q, M * i + cols[c].start, i == 0, i == 7)
+
+        def gate(c, n, engine):
+            f = raw["f" + c][:, 2 * n : 2 * n + 2, :]
+            nc.vector.scalar_tensor_tensor(
+                out=f, in0=raw["zs" + c][:, 2 * n : 2 * n + 2, :], scalar=0.0, in1=f, op0=IS_GT, op1=MULT
+            )
+
+        def second(c, t, engine):
+            nc.vector.tensor_tensor(
+                out=d_sec["ab".index(c)][:, t, :], in0=bank(("dh", c, t))[:], in1=raw["f" + c][:, t, :], op=MULT
+            )
+
+        def inter(c, t, engine):
+            nc.vector.scalar_tensor_tensor(
+                out=d_int["ab".index(c)][:, t, :], in0=raw["zi" + c][:, t, :], scalar=0.0, in1=bank(("dh", c, t))[:],
+                op0=IS_GT, op1=MULT,
+            )
+            emptied(("dh", c, t))
+
+        def store(key, hbm_rows, engine):
+            o = outs.tile([P, H], F32, name="result")
+            copy_on[engine](out=o[:], in_=bank(key)[:])
+            emptied(key)
+            nc.sync.dma_start(out=hbm_rows, in_=o[:])
+
+        def dw(c, n, engine):
+            open_bank(("dw", c, n), [P, H])
+            matmul(bank(("dw", c, n)), dt_q, cols[c].start + P * n, y_q, 0, True, True)
+
+        def dw_out(c, n, engine):
+            r0 = cols[c].start + P * n
+            store(("dw", c, n), out_1[r0 : r0 + P, :], engine)
+
+        def dy(c, t, engine):
+            if c == "a":
+                open_bank(("dy", t), [P, H])
+            for k in (0, 2) if c == "a" else (1, 3):
+                matmul(bank(("dy", t)), df_q, TOK * k + P * t, w1_q, E * k, k == 0, k == 3)
+
+        def dy_out(c, t, engine):
+            store(("dy", t), dy_hbm[:, t, :], engine)
+
+        actions = {
+            "turn": turn, "drain": drain, "pack": pack, "quant": quant, "dh": dh, "gate": gate, "second": second,
+            "int": inter, "dw": dw, "dw_out": dw_out, "dy": dy, "dy_out": dy_out,
+        }
+        for step in STEPS.split():
+            action, what, n, engine = step.replace(".", ":").split(":")
+            actions[action](what, int(n), engine)

@@ -22,32 +22,32 @@ H = 512
 GROUPS = 8
 
 LOADS = """
-y g0 w0a w1 g1 w3 w0b g2 w2 g4 w5 w4 g6 w6 zsb w7 fb zsa fa ws zia wi zib
+w7 gA1 w1 w5 w2 gA0 w0a gB0 w4 w6 w3 gB1 zs1 f1 w0b wi zs0 f0 ws zi0 y zi1
 """
 
 STEPS = """
-pack:y.1:V pack:y.0:S turn:g0.1:T quant:y.0:V pack:w0a.0:V pack:w0a.1:S turn:g0.0:T drain:g0.1:V drain:g0.0:V
-quant:w0a.0:V pack:w1a.0:S pack:w1a.1:V pack:w1b.0:V turn:g1.0:T pack:w1b.1:S quant:g0.0:V turn:g1.1:T
-quant:w1a.0:V drain:g1.0:V pack:w3a.1:S dh:a.0:T quant:w1b.0:V pack:w3b.0:V pack:w3a.0:S pack:w0b.1:V
-pack:w0b.0:V drain:g1.1:S quant:w3a.0:V pack:w3b.1:S turn:g3.0:T quant:g1.0:V turn:g2.0:T quant:w0b.0:V
-drain:g3.0:S dh:a.1:T quant:w3b.0:V drain:g2.0:S pack:w2a.1:V pack:w2b.1:S turn:g3.1:T pack:w2b.0:V pack:w2a.0:V
-turn:g2.1:T drain:g3.1:S quant:w2b.0:V turn:g4.1:T drain:g2.1:S quant:g3.0:V turn:g5.1:T drain:g4.1:S
-quant:g2.0:V turn:g5.0:T drain:g5.1:S quant:w2a.0:V turn:g4.0:T pack:w5b.1:S pack:w5b.0:V pack:w5a.0:V dh:a.2:T
-drain:g4.0:S quant:w5b.0:V pack:w5a.1:S pack:w4a.1:V quant:g4.0:V pack:w4b.1:S dh:a.3:T quant:w5a.0:V
-pack:w4b.0:V pack:w4a.0:S quant:w4b.0:V turn:g6.0:T drain:g5.0:S quant:w4a.0:V turn:g6.1:T drain:g6.0:V
-pack:w6b.1:S dh:a.4:T pack:w6a.0:V pack:w6a.1:V pack:w6b.0:S turn:g7.1:T quant:g5.0:V turn:g7.0:T quant:w6a.0:V
-drain:g6.1:S dh:a.5:T quant:w6b.0:V drain:g7.0:S quant:g6.0:V drain:g7.1:S quant:g7.0:V dh:b.0:T pack:w7a.0:S
-pack:w7b.1:V dh:a.6:T gate:b.0:V pack:w7b.0:S dh:b.1:T gate:b.1:V pack:w7a.1:S dh:b.2:T quant:w7b.0:V
-quant:w7a.0:V dh:b.3:T gate:a.0:V dh:a.7:T gate:a.1:V pack:s1.1:S dh:b.4:T pack:s0.1:G second:a.1:V second:a.2:V
-dh:b.5:T pack:s0.0:S second:a.0:V second:a.3:V dh:b.6:T pack:s1.0:S pack:ta.1:G int:a.2:V int:a.1:V dh:b.7:T
-pack:ta.0:S int:a.0:V pack:i0.1:G int:a.3:V turn:dia.0:T second:b.0:V pack:i1.1:S turn:dsa.0:T second:b.3:V
-turn:dsa.1:T pack:i0.0:G second:b.1:V turn:dia.1:T drain:dsa.1:S second:b.2:V drain:dia.1:S turn:dsb.0:T
-pack:tb.1:G int:b.0:V pack:tb.0:S turn:dsb.1:T int:b.2:V int:b.3:V drain:dia.0:S quant:ta.0:V turn:dib.1:T
-drain:dsa.0:S quant:tb.0:V pack:i1.0:S dw:a.1:T quant:s0.0:V dw:b.3:T quant:dia.0:V drain:dsb.1:S dw:a.2:T
-quant:i0.0:V dw_out:b.3:S dw:b.2:T int:b.1:V drain:dib.1:S dw:a.0:T dw:b.1:T quant:dsa.0:V dw_out:a.0:S
-turn:dib.0:T dw_out:a.2:S quant:s1.0:V dy:a.3:T dw_out:b.2:S drain:dsb.0:V dy:a.0:T dw_out:a.1:S quant:i1.0:V
-dw:a.3:T drain:dib.0:S dy:a.1:T quant:dsb.0:V dw_out:a.3:S dw:b.0:T quant:dib.0:V dy:a.2:T dw_out:b.1:S
-dw_out:b.0:V dy:b.1:T dy:b.3:T dy_out:b.1:S dy:b.2:T dy_out:b.3:S dy:b.0:T dy_out:b.2:S dy_out:b.0:V
+pack:w7b.0:V pack:w7a.1:S pack:w7b.1:V pack:w7a.0:S quant:w7b.0:V turn:g1.1:T quant:w7a.0:V turn:g2.1:T
+drain:g1.1:S pack:w1b.0:V pack:w1b.1:S turn:g0.1:T drain:g2.1:V turn:g3.1:T drain:g0.1:S pack:w1a.0:V
+quant:w1b.0:V pack:w5b.0:S pack:w1a.1:V drain:g3.1:V pack:w5a.0:S quant:w1a.0:V pack:w2b.0:V pack:w5a.1:S
+pack:w2b.1:V pack:w2a.0:V pack:w5b.1:S quant:w5a.0:V turn:g1.0:T quant:w2b.0:V pack:w2a.1:S quant:w5b.0:V
+turn:g0.0:T pack:w0a.0:V pack:w0a.1:S turn:g2.0:T quant:w2a.0:V drain:g1.0:S quant:w0a.0:V turn:g3.0:T
+drain:g0.0:S quant:g1.0:V drain:g2.0:S quant:g0.0:V turn:g7.0:T drain:g3.0:S quant:g2.0:V turn:g4.0:T
+drain:g7.0:S quant:g3.0:V pack:w4b.0:S pack:w4b.1:V turn:g6.0:T drain:g4.0:V pack:w4a.0:S quant:w4b.0:V dh:a.0:T
+pack:w6b.0:V pack:w4a.1:S pack:w6b.1:V pack:w6a.0:V dh:a.1:T drain:g6.0:S quant:w4a.0:V pack:w3a.0:S
+quant:w6b.0:V dh:a.2:T pack:w3a.1:V pack:w3b.0:S pack:w6a.1:V turn:g5.0:T turn:g6.1:T quant:w3a.0:V drain:g5.0:S
+turn:g4.1:T quant:w6a.0:V drain:g6.1:S turn:g7.1:T drain:g4.1:S quant:g6.0:V turn:g5.1:T drain:g7.1:S
+quant:g4.0:V dh:a.3:T drain:g5.1:S quant:g7.0:V pack:w3b.1:S quant:g5.0:V dh:a.4:T gate:a.1:V pack:w0b.1:S
+gate:b.1:V dh:a.5:T pack:w0b.0:S quant:w3b.0:V dh:a.6:T pack:i1.0:V pack:i0.1:S pack:i1.1:V dh:a.7:T
+quant:w0b.0:V pack:i0.0:S quant:i1.0:V dh:b.0:T second:a.2:V dh:b.1:T quant:i0.0:V gate:a.0:V dh:b.2:T
+gate:b.0:V dh:b.3:T pack:s1.0:S pack:s0.0:G second:a.1:V dh:b.4:T second:a.0:V pack:s0.1:S second:a.3:V dh:b.5:T
+pack:ta.0:G int:a.0:V pack:ta.1:S int:a.1:V turn:dsa.1:T quant:s0.0:V turn:dia.0:T pack:y.0:S pack:y.1:V
+dh:b.6:T quant:ta.0:V drain:dia.0:S quant:y.0:V dh:b.7:T pack:s1.1:S int:a.2:V dw:a.3:T int:a.3:V drain:dsa.1:S
+turn:dsa.0:T second:b.2:V dw_out:a.3:S turn:dia.1:T second:b.3:V drain:dsa.0:S dw:a.1:T second:b.0:V dw:a.2:T
+drain:dia.1:S turn:dsb.1:T quant:dsa.0:V dw_out:a.1:S dw:a.0:T quant:dia.0:V dw_out:a.2:S second:b.1:V
+drain:dsb.1:S dy:a.0:T pack:tb.1:G pack:tb.0:S int:b.0:V dy:a.1:T int:b.1:V turn:dsb.0:T int:b.3:V turn:dib.0:T
+dw_out:a.0:S quant:tb.0:V drain:dsb.0:S dy:a.2:T int:b.2:V drain:dib.0:S dw:b.0:T dw:b.1:T dw_out:b.0:S
+quant:dsb.0:V turn:dib.1:T dw_out:b.1:S quant:s1.0:V dw:b.3:T drain:dib.1:S dy:a.3:T dw_out:b.3:S quant:dib.0:V
+dw:b.2:T dw_out:b.2:V dy:b.2:T dy:b.3:T dy_out:b.2:S dy:b.1:T dy_out:b.3:V dy:b.0:T dy_out:b.1:V dy_out:b.0:S
 """
 
 
@@ -63,8 +63,8 @@ def tile_smcrossbaby_1_pb_v_kernel(
 
     with ExitStack() as ctx:
         keep = ctx.enter_context(tc.tile_pool(name="keep", bufs=1))
-        big = ctx.enter_context(tc.tile_pool(name="big", bufs=7))
-        small = ctx.enter_context(tc.tile_pool(name="small", bufs=7))
+        big = ctx.enter_context(tc.tile_pool(name="big", bufs=8))
+        small = ctx.enter_context(tc.tile_pool(name="small", bufs=5))
         outs = ctx.enter_context(tc.tile_pool(name="outs", bufs=6))
         psum = ctx.enter_context(tc.psum_pool(name="psum", bufs=1))
 
@@ -94,20 +94,20 @@ def tile_smcrossbaby_1_pb_v_kernel(
         cols = {"a": slice(0, H), "b": slice(H, M)}
 
         hbm = {"y": y_hbm, "ws": ws_hbm, "wi": wi_hbm}
-        for k in (0, 1):
-            hbm[f"g{k}"] = g_hbm[:, :, H * k : H * (k + 1)]
-        for k in (2, 4, 6):
-            hbm[f"g{k}"] = g_hbm[:, :, H * k : H * (k + 2)]
+        for h in range(2):
+            pair = slice(2 * h, 2 * h + 2)
+            hbm[f"gA{h}"] = g_hbm[:, pair, 0 : V // 2]
+            hbm[f"gB{h}"] = g_hbm[:, pair, V // 2 : V]
+            hbm[f"f{h}"] = f_hbm[:, pair]
+            hbm[f"zs{h}"] = zs_hbm[:, pair]
+            hbm[f"zi{h}"] = zi_hbm[:, pair]
         for i in range(1, 8):
             hbm[f"w{i}"] = w_hbm[:, i]
         for c in "ab":
             hbm["w0" + c] = w_hbm[:, 0, :, cols[c]]
-            hbm["f" + c] = f_hbm[:, :, cols[c]]
-            hbm["zs" + c] = zs_hbm[:, :, cols[c]]
-            hbm["zi" + c] = zi_hbm[:, :, cols[c]]
         raw = {}
         for n in LOADS.split():
-            half_size = n in ("g0", "g1", "w0a", "w0b", "y", "fa", "fb")
+            half_size = n in ("w0a", "w0b", "y", "f0", "f1")
             pool = small if half_size else big
             raw[n] = pool.tile(list(hbm[n].shape), hbm[n].dtype, name="raw_" + n, tag="raw", align_bytes=64)
             nc.sync.dma_start(out=raw[n][:], in_=hbm[n])
@@ -119,14 +119,17 @@ def tile_smcrossbaby_1_pb_v_kernel(
             for i in range(8):
                 rows_of[f"w{i}{c}"] = raw["w0" + c][:] if i == 0 else raw[f"w{i}"][:, :, cols[c]]
                 dest[f"w{i}{c}"] = (w_q, M * i + H * h, E4M3)
-            words_of["ds" + c] = d_sec[h][:].bitcast(F32)
-            words_of["di" + c] = d_int[h][:].bitcast(F32)
+            for n in range(2):
+                pair = slice(2 * n, 2 * n + 2)
+                words_of["ds" + c, n] = d_sec[h][:].bitcast(F32)[:, pair]
+                words_of["di" + c, n] = d_int[h][:].bitcast(F32)[:, pair]
             dest["ds" + c] = (df_q, TOK * h, E5M2)
             dest["di" + c] = (df_q, TOK * (2 + h), E5M2)
             dest["t" + c] = (dt_q, H * h, E5M2)
         for k in range(8):
-            words = raw[f"g{k}"][:] if k < 2 else raw[f"g{k - k % 2}"][:, :, H * (k % 2) : H * (k % 2 + 1)]
-            words_of[f"g{k}"] = words.bitcast(F32)
+            for n in range(2):
+                words = raw[("gA" if k < 4 else "gB") + str(n)][:].bitcast(F32)
+                words_of[f"g{k}", n] = words[:, :, 256 * (k % 4) : 256 * (k % 4 + 1)]
             dest[f"g{k}"] = (g_q, TOK * k, E5M2)
         for k in range(2):
             rows_of[f"s{k}"] = raw["ws"][:, k]
@@ -176,7 +179,7 @@ def tile_smcrossbaby_1_pb_v_kernel(
             for j in range(2):
                 for u in range(2):
                     nc.tensor.transpose(
-                        bank(("turn", what, n))[:, j, u, :], words_of[what][:, 2 * n + j, u : 256 : 2], ident[:]
+                        bank(("turn", what, n))[:, j, u, :], words_of[what, n][:, j, u : 256 : 2], ident[:]
                     )
 
         def drain(what, n, engine):
@@ -212,19 +215,19 @@ def tile_smcrossbaby_1_pb_v_kernel(
                 matmul(bank(("dh", c, t)), g_q, TOK * i + P * t, w_q, M * i + cols[c].start, i == 0, i == 7)
 
         def gate(c, n, engine):
-            f = raw["f" + c][:, 2 * n : 2 * n + 2, :]
+            f = raw[f"f{n}"][:, :, cols[c]]
             nc.vector.scalar_tensor_tensor(
-                out=f, in0=raw["zs" + c][:, 2 * n : 2 * n + 2, :], scalar=0.0, in1=f, op0=IS_GT, op1=MULT
+                out=f, in0=raw[f"zs{n}"][:, :, cols[c]], scalar=0.0, in1=f, op0=IS_GT, op1=MULT
             )
 
         def second(c, t, engine):
             nc.vector.tensor_tensor(
-                out=d_sec["ab".index(c)][:, t, :], in0=bank(("dh", c, t))[:], in1=raw["f" + c][:, t, :], op=MULT
+                out=d_sec["ab".index(c)][:, t, :], in0=bank(("dh", c, t))[:], in1=raw[f"f{t // 2}"][:, t % 2, cols[c]], op=MULT
             )
 
         def inter(c, t, engine):
             nc.vector.scalar_tensor_tensor(
-                out=d_int["ab".index(c)][:, t, :], in0=raw["zi" + c][:, t, :], scalar=0.0, in1=bank(("dh", c, t))[:],
+                out=d_int["ab".index(c)][:, t, :], in0=raw[f"zi{t // 2}"][:, t % 2, cols[c]], scalar=0.0, in1=bank(("dh", c, t))[:],
                 op0=IS_GT, op1=MULT,
             )
             emptied(("dh", c, t))

from contextlib import ExitStack

import concourse.mybir as mybir
from concourse.masks import make_identity

TOK, V, E, M = 512, 4096, 512, 1024
FLOPS = 2 * (TOK * V * M + TOK * 2 * M * E + M * TOK * E)
BYTES = 2 * (TOK * E + TOK * M + 2 * M * E + V * M + TOK * V) + 4 * (2 * TOK * M + TOK * E + M * E)

F32 = mybir.dt.float32
BF16 = mybir.dt.bfloat16
U32 = mybir.dt.uint32
U8 = mybir.dt.uint8
E4M3 = mybir.dt.float8_e4m3fn_x4
E5M2 = mybir.dt.float8_e5m2_x4
MULT = mybir.AluOpType.mult
ADD = mybir.AluOpType.add
IS_GT = mybir.AluOpType.is_gt

P = 128
H = 512
GROUPS = 8

LOADS = """
w7 gA1 w1 w5 w2 gA0 w0a gB0 w4 w6 w3 gB1 zs1 f1 w0b wi zs0 f0 ws zi0 y zi1
"""

STEPS = """
pack:w7b.0:V pack:w7a.1:S pack:w7b.1:V pack:w7a.0:S quant:w7b.0:V turn:g1.1:T quant:w7a.0:V turn:g2.1:T
drain:g1.1:S pack:w1b.0:V pack:w1b.1:S turn:g0.1:T drain:g2.1:V turn:g3.1:T drain:g0.1:S pack:w1a.0:V
quant:w1b.0:V pack:w5b.0:S pack:w1a.1:V drain:g3.1:V pack:w5a.0:S quant:w1a.0:V pack:w2b.0:V pack:w5a.1:S
pack:w2b.1:V pack:w2a.0:V pack:w5b.1:S quant:w5a.0:V turn:g1.0:T quant:w2b.0:V pack:w2a.1:S quant:w5b.0:V
turn:g0.0:T pack:w0a.0:V pack:w0a.1:S turn:g2.0:T quant:w2a.0:V drain:g1.0:S quant:w0a.0:V turn:g3.0:T
drain:g0.0:S quant:g1.0:V drain:g2.0:S quant:g0.0:V turn:g7.0:T drain:g3.0:S quant:g2.0:V turn:g4.0:T
drain:g7.0:S quant:g3.0:V pack:w4b.0:S pack:w4b.1:V turn:g6.0:T drain:g4.0:V pack:w4a.0:S quant:w4b.0:V dh:a.0:T
pack:w6b.0:V pack:w4a.1:S pack:w6b.1:V pack:w6a.0:V dh:a.1:T drain:g6.0:S quant:w4a.0:V pack:w3a.0:S
quant:w6b.0:V dh:a.2:T pack:w3a.1:V pack:w3b.0:S pack:w6a.1:V turn:g5.0:T turn:g6.1:T quant:w3a.0:V drain:g5.0:S
turn:g4.1:T quant:w6a.0:V drain:g6.1:S turn:g7.1:T drain:g4.1:S quant:g6.0:V turn:g5.1:T drain:g7.1:S
quant:g4.0:V dh:a.3:T drain:g5.1:S quant:g7.0:V pack:w3b.1:S quant:g5.0:V dh:a.4:T gate:a.1:V pack:w0b.1:S
gate:b.1:V dh:a.5:T pack:w0b.0:S quant:w3b.0:V dh:a.6:T pack:i1.0:V pack:i0.1:S pack:i1.1:V dh:a.7:T
quant:w0b.0:V pack:i0.0:S quant:i1.0:V dh:b.0:T second:a.2:V dh:b.1:T quant:i0.0:V gate:a.0:V dh:b.2:T
gate:b.0:V dh:b.3:T pack:s1.0:S pack:s0.0:G second:a.1:V dh:b.4:T second:a.0:V pack:s0.1:S second:a.3:V dh:b.5:T
pack:ta.0:G int:a.0:V pack:ta.1:S int:a.1:V turn:dsa.1:T quant:s0.0:V turn:dia.0:T pack:y.0:S pack:y.1:V
dh:b.6:T quant:ta.0:V drain:dia.0:S quant:y.0:V dh:b.7:T pack:s1.1:S int:a.2:V dw:a.3:T int:a.3:V drain:dsa.1:S
turn:dsa.0:T second:b.2:V dw_out:a.3:S turn:dia.1:T second:b.3:V drain:dsa.0:S dw:a.1:T second:b.0:V dw:a.2:T
drain:dia.1:S turn:dsb.1:T quant:dsa.0:V dw_out:a.1:S dw:a.0:T quant:dia.0:V dw_out:a.2:S second:b.1:V
drain:dsb.1:S dy:a.0:T pack:tb.1:G pack:tb.0:S int:b.0:V dy:a.1:T int:b.1:V turn:dsb.0:T int:b.3:V turn:dib.0:T
dw_out:a.0:S quant:tb.0:V drain:dsb.0:S dy:a.2:T int:b.2:V drain:dib.0:S dw:b.0:T dw:b.1:T dw_out:b.0:S
quant:dsb.0:V turn:dib.1:T dw_out:b.1:S quant:s1.0:V dw:b.3:T drain:dib.1:S dy:a.3:T dw_out:b.3:S quant:dib.0:V
dw:b.2:T dw_out:b.2:V dy:b.2:T dy:b.3:T dy_out:b.2:S dy:b.1:T dy_out:b.3:V dy:b.0:T dy_out:b.1:V dy_out:b.0:S
"""


def tile_smcrossbaby_1_pb_v_kernel(
    tc, y2, first, w_second, b_second, w_int, b_int, w_out, b_out, z_second, z_int, grad_out, out_0, out_1
):
    nc = tc.nc

    def gpsimd_copy(out, in_):
        nc.gpsimd.tensor_scalar(out=out, in0=in_, scalar1=1.0, scalar2=0.0, op0=MULT, op1=ADD)

    copy_on = {"V": nc.vector.tensor_copy, "S": nc.scalar.copy, "G": gpsimd_copy}

    with ExitStack() as ctx:
        keep = ctx.enter_context(tc.tile_pool(name="keep", bufs=1))
        big = ctx.enter_context(tc.tile_pool(name="big", bufs=8))
        small = ctx.enter_context(tc.tile_pool(name="small", bufs=5))
        outs = ctx.enter_context(tc.tile_pool(name="outs", bufs=6))
        psum = ctx.enter_context(tc.psum_pool(name="psum", bufs=1))

        ident = keep.tile([P, P], F32, name="ident")
        make_identity(nc, ident[:])
        ctx.enter_context(tc.manual_schedule())

        def codes_and_scales(name, width):
            codes = keep.tile([P, width], U32, name=name + "_codes", align_bytes=64)
            scales = keep.tile([P, width], U8, name=name + "_scales", align_bytes=64)
            return codes, scales

        w_q = codes_and_scales("w", 8 * M)
        g_q = codes_and_scales("g", 8 * TOK)
        y_q = codes_and_scales("y", E)
        w1_q = codes_and_scales("w1", 4 * E)
        dt_q = codes_and_scales("dt", M)
        df_q = codes_and_scales("df", 4 * TOK)
        d_sec = [keep.tile([P, 4, H], BF16, name=f"d_sec{h}", align_bytes=64) for h in range(2)]
        d_int = [keep.tile([P, 4, H], BF16, name=f"d_int{h}", align_bytes=64) for h in range(2)]

        by_token = "(p j) c -> p j c"
        g_hbm, y_hbm, f_hbm, zs_hbm, zi_hbm, dy_hbm = (
            x.rearrange(by_token, j=4) for x in (grad_out, y2, first, z_second, z_int, out_0)
        )
        w_hbm, ws_hbm, wi_hbm = (x.rearrange("(k p j) c -> p k j c", p=P, j=4) for x in (w_out, w_second, w_int))
        cols = {"a": slice(0, H), "b": slice(H, M)}

        hbm = {"y": y_hbm, "ws": ws_hbm, "wi": wi_hbm}
        for h in range(2):
            pair = slice(2 * h, 2 * h + 2)
            hbm[f"gA{h}"] = g_hbm[:, pair, 0 : V // 2]
            hbm[f"gB{h}"] = g_hbm[:, pair, V // 2 : V]
            hbm[f"f{h}"] = f_hbm[:, pair]
            hbm[f"zs{h}"] = zs_hbm[:, pair]
            hbm[f"zi{h}"] = zi_hbm[:, pair]
        for i in range(1, 8):
            hbm[f"w{i}"] = w_hbm[:, i]
        for c in "ab":
            hbm["w0" + c] = w_hbm[:, 0, :, cols[c]]
        raw = {}
        for n in LOADS.split():
            half_size = n in ("w0a", "w0b", "y", "f0", "f1")
            pool = small if half_size else big
            raw[n] = pool.tile(list(hbm[n].shape), hbm[n].dtype, name="raw_" + n, tag="raw", align_bytes=64)
            nc.sync.dma_start(out=raw[n][:], in_=hbm[n])

        rows_of = {"y": raw["y"][:], "ta": d_sec[0][:], "tb": d_sec[1][:]}
        words_of = {}
        dest = {"y": (y_q, 0, E4M3)}
        for h, c in enumerate("ab"):
            for i in range(8):
                rows_of[f"w{i}{c}"] = raw["w0" + c][:] if i == 0 else raw[f"w{i}"][:, :, cols[c]]
                dest[f"w{i}{c}"] = (w_q, M * i + H * h, E4M3)
            for n in range(2):
                pair = slice(2 * n, 2 * n + 2)
                words_of["ds" + c, n] = d_sec[h][:].bitcast(F32)[:, pair]
                words_of["di" + c, n] = d_int[h][:].bitcast(F32)[:, pair]
            dest["ds" + c] = (df_q, TOK * h, E5M2)
            dest["di" + c] = (df_q, TOK * (2 + h), E5M2)
            dest["t" + c] = (dt_q, H * h, E5M2)
        for k in range(8):
            for n in range(2):
                words = raw[("gA" if k < 4 else "gB") + str(n)][:].bitcast(F32)
                words_of[f"g{k}", n] = words[:, :, 256 * (k % 4) : 256 * (k % 4 + 1)]
            dest[f"g{k}"] = (g_q, TOK * k, E5M2)
        for k in range(2):
            rows_of[f"s{k}"] = raw["ws"][:, k]
            rows_of[f"i{k}"] = raw["wi"][:, k]
            dest[f"s{k}"] = (w1_q, E * k, E4M3)
            dest[f"i{k}"] = (w1_q, E * (2 + k), E4M3)

        free_banks = list(range(8))
        free_groups = list(range(GROUPS))
        in_bank = {}
        group = {}
        group_slot = {}

        def open_bank(key, shape):
            n = free_banks[0]
            free_banks.remove(n)
            in_bank[key] = (psum.tile(shape, F32, name=f"bank{n}", tag=f"bank{n}"), n)

        def emptied(key):
            tile, n = in_bank[key]
            free_banks.append(n)

        def bank(key):
            return in_bank[key][0]

        def group_of(key):
            if key not in group:
                n = free_groups[0]
                free_groups.remove(n)
                group_slot[key] = n
                group[key] = keep.tile([P, 4 * H], BF16, name=f"group{n}", tag=f"group{n}", align_bytes=64)
            return group[key]

        def matmul(out, lhs, l0, rhs, r0, start, stop):
            nc.tensor.matmul_mx(
                out=out[:],
                lhsT=lhs[0][:, l0 : l0 + P].bitcast(E5M2),
                lhsT_scale=lhs[1][:, l0 : l0 + P],
                rhs=rhs[0][:, r0 : r0 + H].bitcast(E4M3),
                rhs_scale=rhs[1][:, r0 : r0 + H],
                start=start,
                stop=stop,
            )

        def turn(what, n, engine):
            open_bank(("turn", what, n), [P, 2, 2, P])
            for j in range(2):
                for u in range(2):
                    nc.tensor.transpose(
                        bank(("turn", what, n))[:, j, u, :], words_of[what, n][:, j, u : 256 : 2], ident[:]
                    )

        def drain(what, n, engine):
            dst = group_of(what)[:, 2 * H * n : 2 * H * (n + 1)].bitcast(F32)
            copy_on[engine](
                out=dst.rearrange("p (j r u) -> p j r u", j=2, u=2),
                in_=bank(("turn", what, n))[:].rearrange("p j u r -> p j r u"),
            )
            emptied(("turn", what, n))

        def pack(what, n, engine):
            c0 = 256 * n
            src = rows_of[what][:, :, c0 : c0 + 256]
            dst = group_of(what)[:, 4 * c0 : 4 * (c0 + 256)]
            if engine == "G":
                gpsimd_copy(out=dst.rearrange("p (c t) -> p c t", t=4), in_=src.rearrange("p t c -> p c t"))
            else:
                copy_on[engine](
                    out=dst.rearrange("p (c i t) -> p c t i", i=4, t=4), in_=src.rearrange("p t (c i) -> p c t i", i=4)
                )

        def quant(what, n, engine):
            q, c0, fmt = dest[what]
            nc.vector.quantize_mx(
                out=q[0][:, c0 : c0 + H].bitcast(fmt), scales=q[1][:, c0 : c0 + H], in_=group[what][:]
            )
            free_groups.append(group_slot[what])

        def dh(c, i, engine):
            for t in range(4):
                if i == 0:
                    open_bank(("dh", c, t), [P, H])
                matmul(bank(("dh", c, t)), g_q, TOK * i + P * t, w_q, M * i + cols[c].start, i == 0, i == 7)

        def gate(c, n, engine):
            f = raw[f"f{n}"][:, :, cols[c]]
            nc.vector.scalar_tensor_tensor(
                out=f, in0=raw[f"zs{n}"][:, :, cols[c]], scalar=0.0, in1=f, op0=IS_GT, op1=MULT
            )

        def second(c, t, engine):
            nc.vector.tensor_tensor(
                out=d_sec["ab".index(c)][:, t, :], in0=bank(("dh", c, t))[:], in1=raw[f"f{t // 2}"][:, t % 2, cols[c]], op=MULT
            )

        def inter(c, t, engine):
            nc.vector.scalar_tensor_tensor(
                out=d_int["ab".index(c)][:, t, :], in0=raw[f"zi{t // 2}"][:, t % 2, cols[c]], scalar=0.0, in1=bank(("dh", c, t))[:],
                op0=IS_GT, op1=MULT,
            )
            emptied(("dh", c, t))

        def store(key, hbm_rows, engine):
            o = outs.tile([P, H], F32, name="result")
            copy_on[engine](out=o[:], in_=bank(key)[:])
            emptied(key)
            nc.sync.dma_start(out=hbm_rows, in_=o[:])

        def dw(c, n, engine):
            open_bank(("dw", c, n), [P, H])
            matmul(bank(("dw", c, n)), dt_q, cols[c].start + P * n, y_q, 0, True, True)

        def dw_out(c, n, engine):
            r0 = cols[c].start + P * n
            store(("dw", c, n), out_1[r0 : r0 + P, :], engine)

        def dy(c, t, engine):
            if c == "a":
                open_bank(("dy", t), [P, H])
            for k in (0, 2) if c == "a" else (1, 3):
                matmul(bank(("dy", t)), df_q, TOK * k + P * t, w1_q, E * k, k == 0, k == 3)

        def dy_out(c, t, engine):
            store(("dy", t), dy_hbm[:, t, :], engine)

        actions = {
            "turn": turn, "drain": drain, "pack": pack, "quant": quant, "dh": dh, "gate": gate, "second": second,
            "int": inter, "dw": dw, "dw_out": dw_out, "dy": dy, "dy_out": dy_out,
        }
        for step in STEPS.split():
            action, what, n, engine = step.replace(".", ":").split(":")
            actions[action](what, int(n), engine)
